import numpy as np
import ml_dtypes


def mxq(x, axis, fmt="e4m3"):
    dtype, down = {"e4m3": (ml_dtypes.float8_e4m3fn, 7), "e5m2": (ml_dtypes.float8_e5m2, 14)}[fmt]
    v = np.moveaxis(np.asarray(x, np.float32).astype(ml_dtypes.bfloat16).astype(np.float64), axis, -1)
    blocks = v.reshape(v.shape[:-1] + (-1, 32))
    amax = np.abs(blocks).max(-1, keepdims=True)
    byte = np.maximum(np.where(amax > 0, np.frexp(amax)[1] - 1 + 127, 0) - down, 1)
    scale = np.exp2(byte - 127.0)
    codes = (blocks / scale).astype(np.float32).astype(dtype).astype(np.float64)
    return np.moveaxis((codes * scale).reshape(v.shape), -1, axis)


WIDE = False


def mx_kscale(k):
    if not WIDE:
        return np.ones(k)
    levels = np.array([10, -10, 5, -5, 0])
    if k % 512:
        return np.exp2(np.random.permutation(np.resize(levels, k // 32))).repeat(32)
    a = np.empty((k // 512, 16))
    for p in range(k // 512):
        a[p, :8] = np.random.permutation(np.resize(levels, 8))
        for g in range(8):
            far = levels[np.abs(levels - a[p, g]) >= 10]
            a[p, g + 8] = far[np.random.randint(len(far))]
    return np.exp2(a.ravel()).repeat(32)


BF16 = ml_dtypes.bfloat16


def bf(x):
    return np.asarray(x, np.float32).astype(BF16)


def f64(x):
    return np.asarray(x).astype(np.float64)


B, T, C, QLR, H, R, KVL, VD = 4, 1024, 1024, 1536, 4, 128, 512, 128
THETA = 10000.0
EPS = 1e-6
HALF = R // 2


def rms_norm(v, w):
    return v / np.sqrt(np.mean(v * v, axis=-1, keepdims=True) + EPS) * w


def rope_cos_sin():
    inv = 1.0 / THETA ** (np.arange(HALF) / HALF)
    ang = np.arange(T)[:, None] * inv
    return np.cos(ang), np.sin(ang)


def apply_rot(v, cos, sin):
    vr, vi = v[..., 0::2], v[..., 1::2]
    c = cos[None, :, None, :]
    s = sin[None, :, None, :]
    return np.stack([vr * c - vi * s, vr * s + vi * c], axis=-1).reshape(v.shape)


def setup_inputs():
    s, t = mx_kscale(C), mx_kscale(KVL)
    return {"x": bf(np.random.standard_normal((B, T, C)) * s),
            "w_kva": bf(np.random.standard_normal((KVL + R, C)) / np.sqrt(C) / s),
            "kva_norm_w": bf((1.0 + 0.1 * np.random.standard_normal(KVL)) * t),
            "w_kvb": bf(np.random.standard_normal((H * (R + VD), KVL)) / np.sqrt(KVL) / t)}


def reference(x, w_kva, kva_norm_w, w_kvb):
    kv_a = mxq(f64(x), 2, "e4m3") @ mxq(f64(w_kva), 1, "e4m3").T
    kv_c = rms_norm(kv_a[..., :KVL], f64(kva_norm_w))
    k_rope_raw = kv_a[..., KVL:]
    kv = (mxq(kv_c, 2, "e4m3") @ mxq(f64(w_kvb), 1, "e4m3").T).reshape(B, T, H, R + VD)
    k_content, v = kv[..., :R], kv[..., R:]
    k_rope = np.broadcast_to(k_rope_raw[:, :, None, :], (B, T, H, R))
    cos, sin = rope_cos_sin()
    k = np.concatenate([k_content, apply_rot(k_rope, cos, sin)], axis=-1)
    return k, v

@@ -1,0 +1,380 @@
+import math
+
+import concourse.mybir as mybir
+from concourse.masks import make_identity
+
+F32 = mybir.dt.float32
+BF16 = mybir.dt.bfloat16
+I32 = mybir.dt.int32
+U32 = mybir.dt.uint32
+U8 = mybir.dt.uint8
+FP8X4 = mybir.dt.float8_e4m3fn_x4
+ALU = mybir.AluOpType
+ACT = mybir.ActivationFunctionType
+
+P = 128
+B, T, C = 4, 1024, 1024
+KVL, R, H = 512, 128, 4
+TPP = 8
+N_PAIRS = B * TPP // 2
+EPS = 1e-6
+RATIO = 10000.0 ** (-1.0 / 64.0)
+
+FLOPS = 2 * B * T * C * (KVL + R) + 2 * B * T * KVL * (H * 256)
+
+
+def tile_multiheadlatentattention_pb_t_kernel(tc, x, w_kva, kva_norm_w, w_kvb, out_0, out_1):
+    nc = tc.nc
+    with tc.tile_pool(name="const", bufs=1) as const, tc.tile_pool(name="xin", bufs=8) as xin, tc.tile_pool(
+        name="stage", bufs=3
+    ) as stage, tc.tile_pool(name="ring", bufs=7) as ring, tc.tile_pool(name="work", bufs=3) as work, tc.tile_pool(
+        name="small", bufs=4
+    ) as small, tc.psum_pool(name="psum", bufs=1) as psum, tc.manual_schedule():
+        state = {"k": 0}
+
+        def k_bank(shape, dtype, name):
+            tag = "K%d" % (state["k"] % 4)
+            state["k"] = state["k"] + 1
+            return psum.tile(shape, dtype, name=name, tag=tag)
+
+        engines = {"S": nc.scalar.copy, "V": nc.vector.tensor_copy}
+
+        g_bc = const.tile([P, KVL], BF16, name="g_bc")
+
+        waq = const.tile([P, 2 * 640], U32, name="waq", align_bytes=64)
+        was = const.tile([P, 2 * 640], U8, name="was", align_bytes=64)
+        wbq = const.tile([P, 1024], U32, name="wbq", align_bytes=64)
+        wbs = const.tile([P, 1024], U8, name="wbs", align_bytes=64)
+        tab1 = const.tile([P, TPP, 2, 64], F32, name="tab1")
+        tab2 = const.tile([P, TPP, 2, 64], F32, name="tab2")
+        ident_f = const.tile([P, P], F32, name="ident_f")
+        ident_b = const.tile([P, P], BF16, name="ident_b")
+        eps_t = const.tile([P, 1], F32, name="eps_t")
+        sin_h = const.tile([P, TPP, 64], F32, name="sin_h")
+        sin_q = const.tile([P, TPP, 64], F32, name="sin_q")
+        sq_q = const.tile([P, TPP, 64], F32, name="sq_q")
+        cos_h = const.tile([P, TPP, 64], F32, name="cos_h")
+        sq_h = const.tile([P, TPP, 64], F32, name="sq_h")
+
+        x_rows = x.rearrange("b (p t) k -> b p (t k)", t=TPP)
+        k_rows = out_0.rearrange("b (p t) h d -> b p t (h d)", t=TPP)
+        v_rows = out_1.rearrange("b (p t) h d -> b p t (h d)", t=TPP)
+        x_words = []
+        live = {}
+
+        def transpose_words(src_words):
+            xt = k_bank([P, 512], F32, "xt")
+            for c in range(4):
+                nc.tensor.transpose(
+                    out=xt[:, P * c : P * c + P],
+                    in_=src_words[:, 256 * (c // 2) + c % 2 : 256 * (c // 2) + 256 : 2],
+                    identity=ident_f[:],
+                )
+            return xt
+
+        def copy_words(xt, dst_bf16, eng):
+            engines[eng](
+                out=dst_bf16.bitcast(F32).rearrange("p (g w u) -> p g w u", g=2, u=2),
+                in_=xt[:].rearrange("p (g u w) -> p g w u", g=2, u=2),
+            )
+
+        with tc.tile_pool(name="setup", bufs=1) as setup:
+            g_row = setup.tile([P, KVL], BF16, name="g_row")
+            nc.vector.memset(g_row[:], 0.0)
+            nc.scalar.dma_start(out=g_row[0:1, :], in_=kva_norm_w.rearrange("(o k) -> o k", o=1))
+            ones = setup.tile([P, P], BF16, name="ones")
+            nc.vector.memset(ones[:], 1.0)
+            war = setup.tile([P, 5 * C], BF16, name="war")
+            nc.sync.dma_start(
+                out=war[:, 0 : 4 * C].rearrange("p (t k) -> p t k", t=4),
+                in_=w_kva[0:KVL, :].rearrange("(p t) k -> p t k", t=4),
+            )
+            nc.sync.dma_start(out=war[:, 4 * C : 5 * C], in_=w_kva[KVL : KVL + R, :])
+            wbr = setup.tile([P, 8 * KVL], BF16, name="wbr")
+            nc.sync.dma_start(
+                out=wbr[:].rearrange("p (r k) -> p r k", r=8), in_=w_kvb.rearrange("(r p) k -> p r k", p=P)
+            )
+            for hb in range(8):
+                xr = xin.tile([P, 4 * C], BF16, name="xr", tag="xr")
+                nc.sync.dma_start(out=xr[:], in_=x_rows[hb // 2][:, 4 * C * (hb % 2) : 4 * C * (hb % 2) + 4 * C])
+                x_words.append(xr[:].bitcast(F32))
+
+            pos_i = setup.tile([P, TPP], I32, name="pos_i")
+            nc.gpsimd.iota(pos_i[:], pattern=[[1, TPP]], base=0, channel_multiplier=TPP)
+            make_identity(nc, ident_f[:])
+            make_identity(nc, ident_b[:])
+            nc.vector.memset(eps_t[:], EPS)
+            pos_f = setup.tile([P, TPP], F32, name="pos_f")
+            nc.vector.tensor_copy(out=pos_f[:], in_=pos_i[:])
+            inv = setup.tile([P, 64], F32, name="inv")
+            nc.vector.memset(inv[:, 0:1], 1.0)
+            for s in range(6):
+                n = 2**s
+                nc.vector.tensor_scalar(
+                    out=inv[:, n : 2 * n], in0=inv[:, 0:n], scalar1=RATIO**n, scalar2=None, op0=ALU.mult
+                )
+            turns = setup.tile([P, TPP, 64], F32, name="turns")
+            nc.vector.scalar_tensor_tensor(
+                out=turns[:],
+                in0=pos_f[:].unsqueeze(2).to_broadcast([P, TPP, 64]),
+                scalar=1.0 / (2.0 * math.pi),
+                in1=inv[:].unsqueeze(1).to_broadcast([P, TPP, 64]),
+                op0=ALU.mult,
+                op1=ALU.mult,
+            )
+            whole_i = setup.tile([P, TPP, 64], I32, name="whole_i")
+            nc.vector.tensor_copy(out=whole_i[:], in_=turns[:])
+            whole_f = setup.tile([P, TPP, 64], F32, name="whole_f")
+            nc.vector.tensor_copy(out=whole_f[:], in_=whole_i[:])
+            frac = setup.tile([P, TPP, 64], F32, name="frac")
+            nc.vector.tensor_tensor(out=frac[:], in0=turns[:], in1=whole_f[:], op=ALU.subtract)
+            nc.scalar.activation(out=sin_h[:], in_=frac[:], func=ACT.Sin, scale=math.pi)
+            nc.scalar.activation(out=sin_q[:], in_=frac[:], func=ACT.Sin, scale=0.5 * math.pi)
+
+            war_w = war[:].bitcast(F32)
+            for r in range(5):
+                xt = transpose_words(war_w[:, 512 * r : 512 * r + 512])
+                grp = stage.tile([P, 1024], BF16, name="grp", tag="cgrp", align_bytes=64)
+                copy_words(xt, grp[:], "SV"[r % 2])
+                for g in range(2):
+                    cols = slice(640 * g + P * r, 640 * g + P * r + P)
+                    nc.vector.quantize_mx(
+                        out=waq[:, cols].bitcast(FP8X4), scales=was[:, cols], in_=grp[:, 512 * g : 512 * g + 512]
+                    )
+            wbr_w = wbr[:].bitcast(F32)
+            for n, (ra, rb, dest) in enumerate(((0, 2, 0), (4, 6, 256), (1, 3, 512), (5, 7, 768))):
+                wt = k_bank([P, 512], F32, "wt")
+                for a, r in enumerate((ra, rb)):
+                    for u in range(2):
+                        nc.tensor.transpose(
+                            out=wt[:, 256 * a + P * u : 256 * a + P * u + P],
+                            in_=wbr_w[:, 256 * r + u : 256 * r + 256 : 2],
+                            identity=ident_f[:],
+                        )
+                grp = stage.tile([P, 1024], BF16, name="grp", tag="cgrp", align_bytes=64)
+                copy_words(wt, grp[:], "VS"[n % 2])
+                nc.vector.quantize_mx(
+                    out=wbq[:, dest : dest + 256].bitcast(FP8X4), scales=wbs[:, dest : dest + 256], in_=grp[:]
+                )
+
+            g_ps = k_bank([P, KVL], F32, "g_ps")
+            nc.tensor.matmul(out=g_ps[:], lhsT=ones[:], rhs=g_row[:], start=True, stop=True)
+            nc.scalar.copy(
+                out=g_bc[:].rearrange("p (t m) -> p t m", t=4), in_=g_ps[:].rearrange("p (m t) -> p t m", t=4)
+            )
+
+        def finish_tables():
+            nc.scalar.activation(out=sq_q[:], in_=sin_q[:], func=ACT.Square)
+            nc.scalar.activation(out=cos_h[:], in_=sq_q[:], func=ACT.Copy, scale=-2.0, bias=1.0)
+            nc.scalar.activation(out=sq_h[:], in_=sin_h[:], func=ACT.Square)
+            nc.scalar.activation(out=tab1[:, :, 0, :], in_=sq_h[:], func=ACT.Copy, scale=-2.0, bias=1.0)
+            nc.scalar.activation(out=tab2[:, :, 1, :], in_=sq_h[:], func=ACT.Copy, scale=-2.0, bias=1.0)
+            nc.vector.scalar_tensor_tensor(
+                out=tab1[:, :, 1, :], in0=sin_h[:], scalar=2.0, in1=cos_h[:], op0=ALU.mult, op1=ALU.mult
+            )
+            nc.vector.scalar_tensor_tensor(
+                out=tab2[:, :, 0, :], in0=sin_h[:], scalar=-2.0, in1=cos_h[:], op0=ALU.mult, op1=ALU.mult
+            )
+
+        def x_transpose(q):
+            live["xt", q] = [
+                transpose_words(x_words[(2 * q + a) // 4][:, 512 * ((2 * q + a) % 4) : 512 * ((2 * q + a) % 4) + 512])
+                for a in range(2)
+            ]
+
+        def x_copy(q):
+            xg = stage.tile([P, 2048], BF16, name="xg", tag="xgrp", align_bytes=64)
+            for a in range(2):
+                copy_words(live["xt", q][a], xg[:, 1024 * a : 1024 * a + 1024], "SV"[a])
+            live["xg", q] = xg
+
+        def x_quantise(q):
+            xq = ring.tile([P, 512], U32, name="xq", tag="xq", align_bytes=64)
+            xs = ring.tile([P, 512], U8, name="xs", tag="xs", align_bytes=64)
+            nc.vector.quantize_mx(out=xq[:].bitcast(FP8X4), scales=xs[:], in_=live["xg", q][:])
+            live["xq", q] = (xq, xs)
+
+        def stage1_pass(out, q, a, g, lo, hi):
+            xq, xs = live["xq", q]
+            xc = slice(256 * a + P * g, 256 * a + P * g + P)
+            nc.tensor.matmul_mx(
+                out=out,
+                lhsT=xq[:, xc].bitcast(FP8X4),
+                lhsT_scale=xs[:, xc],
+                rhs=waq[:, 640 * g + lo : 640 * g + hi].bitcast(FP8X4),
+                rhs_scale=was[:, 640 * g + lo : 640 * g + hi],
+                start=(g == 0),
+                stop=(g == 1),
+            )
+
+        def stage1_latent(q):
+            tiles = []
+            for a in range(2):
+                l = psum.tile([P, KVL], F32, name="l", tag="L%d" % a)
+                for g in range(2):
+                    stage1_pass(l[:], q, a, g, 0, KVL)
+                tiles.append(l)
+            live["l", q] = tiles
+
+        def stage1_rotary(q):
+            r_ps = psum.tile([P, 2, R], F32, name="r_ps", tag="R")
+            for a in range(2):
+                for g in range(2):
+                    stage1_pass(r_ps[:, a, :], q, a, g, KVL, KVL + R)
+            live["r", q] = r_ps
+
+        def squares(q):
+            ssq = small.tile([P, 2], F32, name="ssq", tag="ssq")
+            for a in range(2):
+                junk = work.tile([P, KVL], BF16, name="junk", tag="junk", bufs=2)
+                nc.scalar.activation(out=junk[:], in_=live["l", q][a][:], func=ACT.Square, accum_out=ssq[:, a : a + 1])
+            rstd = small.tile([P, 2], F32, name="rstd", tag="rstd")
+            nc.scalar.activation(
+                out=rstd[:], in_=ssq[:], func=ACT.Abs_reciprocal_sqrt, scale=1.0 / KVL, bias=eps_t[:, 0:1]
+            )
+            live["rstd", q] = rstd
+
+        def normalise(q):
+            rstd = live["rstd", q]
+            c_sb = work.tile([P, 2, KVL], BF16, name="c_sb", tag="c_sb")
+            for a in range(2):
+                nc.vector.scalar_tensor_tensor(
+                    out=c_sb[:, a, :],
+                    in0=live["l", q][a][:],
+                    scalar=rstd[:, a : a + 1],
+                    in1=g_bc[:],
+                    op0=ALU.mult,
+                    op1=ALU.mult,
+                )
+            live["c", q] = c_sb
+
+        def c_transpose(q):
+            ct = psum.tile([P, 2, 4, P], BF16, name="ct", tag="C")
+            for a in range(2):
+                for j in range(4):
+                    nc.tensor.transpose(
+                        out=ct[:, a, j, :], in_=live["c", q][:, a, P * j : P * j + P], identity=ident_b[:]
+                    )
+            live["ct", q] = ct
+
+        def c_copy(q):
+            grp = stage.tile([P, 1024], BF16, name="grp", tag="cgrp", align_bytes=64)
+            nc.scalar.copy(
+                out=grp[:].rearrange("p (a w j) -> p a w j", a=2, j=4),
+                in_=live["ct", q][:].rearrange("p a j w -> p a w j"),
+            )
+            live["cg", q] = grp
+
+        def c_quantise(q):
+            cq = work.tile([P, 256], U32, name="cq", tag="cq", align_bytes=64)
+            cs = work.tile([P, 256], U8, name="cs", tag="cs", align_bytes=64)
+            nc.vector.quantize_mx(out=cq[:].bitcast(FP8X4), scales=cs[:], in_=live["cg", q][:])
+            live["cq", q] = (cq, cs)
+
+        def stage2(q):
+            cq, cs = live["cq", q]
+            banks = []
+            for a in range(2):
+                for part in range(2):
+                    kv = k_bank([P, 512], F32, "kv")
+                    nc.tensor.matmul_mx(
+                        out=kv[:],
+                        lhsT=cq[:, P * a : P * a + P].bitcast(FP8X4),
+                        lhsT_scale=cs[:, P * a : P * a + P],
+                        rhs=wbq[:, 512 * part : 512 * part + 512].bitcast(FP8X4),
+                        rhs_scale=wbs[:, 512 * part : 512 * part + 512],
+                        start=True,
+                        stop=True,
+                    )
+                    banks.append(kv)
+            live["kv", q] = banks
+
+        with tc.tile_pool(name="outp", bufs=6) as outp:
+
+            def rotate(q):
+                t0 = 2 * (q % 4)
+                k_sb = outp.tile([P, 2, H, 256], F32, name="k_sb", tag="k_sb")
+                v_sb = outp.tile([P, 2, H * 128], F32, name="v_sb", tag="v_sb")
+                live["out", q] = (k_sb, v_sb)
+                r_pairs = live["r", q][:].rearrange("p t (j e) -> p t e j", e=2)
+                m1 = work.tile([P, 2, 2, 64], F32, name="m1", tag="m1")
+                nc.vector.tensor_tensor(
+                    out=m1[:],
+                    in0=r_pairs[:, :, 0:1, :].to_broadcast([P, 2, 2, 64]),
+                    in1=tab1[:, t0 : t0 + 2, :, :],
+                    op=ALU.mult,
+                )
+                m2 = work.tile([P, 2, 2, 64], F32, name="m2", tag="m2")
+                nc.vector.tensor_tensor(
+                    out=m2[:],
+                    in0=r_pairs[:, :, 1:2, :].to_broadcast([P, 2, 2, 64]),
+                    in1=tab2[:, t0 : t0 + 2, :, :],
+                    op=ALU.mult,
+                )
+                nc.gpsimd.tensor_tensor(
+                    out=k_sb[:, :, 0, 128:256].rearrange("p t (j e) -> p t j e", e=2),
+                    in0=m1[:].rearrange("p t e j -> p t j e"),
+                    in1=m2[:].rearrange("p t e j -> p t j e"),
+                    op=ALU.add,
+                )
+                nc.gpsimd.tensor_scalar(
+                    out=k_sb[:, :, 1:4, 128:256],
+                    in0=k_sb[:, :, 0:1, 128:256].to_broadcast([P, 2, 3, 128]),
+                    scalar1=1.0,
+                    scalar2=0.0,
+                    op0=ALU.mult,
+                    op1=ALU.add,
+                )
+
+            def copy_out(q):
+                k_sb, v_sb = live["out", q]
+                for a in range(2):
+                    eng = engines["SV"[a]]
+                    eng(out=k_sb[:, a, :, 0:128], in_=live["kv", q][2 * a][:].rearrange("p (h d) -> p h d", h=H))
+                    eng(out=v_sb[:, a, :], in_=live["kv", q][2 * a + 1][:])
+
+            def store(q):
+                k_sb, v_sb = live["out", q]
+                b = q // 4
+                t0 = 2 * (q % 4)
+                nc.sync.dma_start(out=k_rows[b][:, t0 : t0 + 2, :], in_=k_sb[:].rearrange("p t h d -> p t (h d)"))
+                nc.sync.dma_start(out=v_rows[b][:, t0 : t0 + 2, :], in_=v_sb[:])
+
+            def is_pair(q):
+                return 0 <= q < N_PAIRS
+
+            x_transpose(0)
+            x_copy(0)
+            x_quantise(0)
+            next_x = 1
+            for n in range(N_PAIRS + 3):
+                fresh = [q for q in range(next_x, next_x + (2 if n < 3 else 1)) if is_pair(q)]
+                next_x = next_x + len(fresh)
+                for q in fresh:
+                    x_transpose(q)
+                if is_pair(n - 2):
+                    c_transpose(n - 2)
+                if is_pair(n - 1):
+                    squares(n - 1)
+                for q in fresh:
+                    x_copy(q)
+                if is_pair(n - 1):
+                    normalise(n - 1)
+                if is_pair(n - 2):
+                    c_copy(n - 2)
+                    c_quantise(n - 2)
+                for q in fresh:
+                    x_quantise(q)
+                if n == 0:
+                    finish_tables()
+                if is_pair(n - 3):
+                    stage2(n - 3)
+                if is_pair(n - 1):
+                    stage1_rotary(n - 1)
+                if is_pair(n):
+                    stage1_latent(n)
+                if is_pair(n - 1):
+                    rotate(n - 1)
+                if is_pair(n - 3):
+                    copy_out(n - 3)
+                    store(n - 3)

@@ -25,209 +25,209 @@ FLOPS = 2 * B * T * C * (KVL + R) + 2 * B * T * KVL * (H * 256)
 
 def tile_multiheadlatentattention_pb_t_kernel(tc, x, w_kva, kva_norm_w, w_kvb, out_0, out_1):
     nc = tc.nc
-    with tc.tile_pool(name="const", bufs=1) as const, tc.tile_pool(name="xin", bufs=8) as xin, tc.tile_pool(
-        name="stage", bufs=3
-    ) as stage, tc.tile_pool(name="ring", bufs=7) as ring, tc.tile_pool(name="work", bufs=3) as work, tc.tile_pool(
-        name="small", bufs=4
-    ) as small, tc.psum_pool(name="psum", bufs=1) as psum, tc.manual_schedule():
-        state = {"k": 0}
-
-        def k_bank(shape, dtype, name):
-            tag = "K%d" % (state["k"] % 4)
-            state["k"] = state["k"] + 1
-            return psum.tile(shape, dtype, name=name, tag=tag)
-
+    with tc.tile_pool(name="const", bufs=1) as const, tc.tile_pool(name="stage", bufs=3) as stage, tc.tile_pool(
+        name="ring", bufs=7
+    ) as ring, tc.tile_pool(name="work", bufs=3) as work, tc.tile_pool(name="small", bufs=4) as small, tc.tile_pool(
+        name="outp", bufs=5
+    ) as outp, tc.psum_pool(name="psum", bufs=1) as psum, tc.manual_schedule():
         engines = {"S": nc.scalar.copy, "V": nc.vector.tensor_copy}
+        live = {}
 
-        g_bc = const.tile([P, KVL], BF16, name="g_bc")
+        def bank(shape, name, tag):
+            return psum.tile(shape, F32, name=name, tag=tag)
 
-        waq = const.tile([P, 2 * 640], U32, name="waq", align_bytes=64)
-        was = const.tile([P, 2 * 640], U8, name="was", align_bytes=64)
-        wbq = const.tile([P, 1024], U32, name="wbq", align_bytes=64)
-        wbs = const.tile([P, 1024], U8, name="wbs", align_bytes=64)
-        tab1 = const.tile([P, TPP, 2, 64], F32, name="tab1")
-        tab2 = const.tile([P, TPP, 2, 64], F32, name="tab2")
-        ident_f = const.tile([P, P], F32, name="ident_f")
-        ident_b = const.tile([P, P], BF16, name="ident_b")
+        pos_i = const.tile([P, TPP], I32, name="pos_i")
+        nc.gpsimd.iota(pos_i[:], pattern=[[1, TPP]], base=0, channel_multiplier=TPP)
+        g_row = const.tile([P, KVL], BF16, name="g_row")
+        nc.gpsimd.memset(g_row[:], 0.0)
+        ident = const.tile([P, P], F32, name="ident")
+        make_identity(nc, ident[:])
+        ones = const.tile([P, P], BF16, name="ones")
+        nc.gpsimd.memset(ones[:], 1.0)
         eps_t = const.tile([P, 1], F32, name="eps_t")
-        sin_h = const.tile([P, TPP, 64], F32, name="sin_h")
-        sin_q = const.tile([P, TPP, 64], F32, name="sin_q")
-        sq_q = const.tile([P, TPP, 64], F32, name="sq_q")
-        cos_h = const.tile([P, TPP, 64], F32, name="cos_h")
-        sq_h = const.tile([P, TPP, 64], F32, name="sq_h")
+        nc.vector.memset(eps_t[:], EPS)
 
         x_rows = x.rearrange("b (p t) k -> b p (t k)", t=TPP)
         k_rows = out_0.rearrange("b (p t) h d -> b p t (h d)", t=TPP)
         v_rows = out_1.rearrange("b (p t) h d -> b p t (h d)", t=TPP)
-        x_words = []
-        live = {}
+        wa_rows = w_kva[0:KVL, :].rearrange("(m s) k -> m s k", s=4)
+        x_words = {}
 
-        def transpose_words(src_words):
-            xt = k_bank([P, 512], F32, "xt")
-            for c in range(4):
-                nc.tensor.transpose(
-                    out=xt[:, P * c : P * c + P],
-                    in_=src_words[:, 256 * (c // 2) + c % 2 : 256 * (c // 2) + 256 : 2],
-                    identity=ident_f[:],
-                )
-            return xt
+        def load_x(q, pairs):
+            xr = const.tile([P, 2 * pairs * C], BF16, name="x_%d" % q)
+            nc.sync.dma_start(out=xr[:], in_=x_rows[q // 4][:, 2 * C * (q % 4) : 2 * C * (q % 4 + pairs)])
+            words = xr[:].bitcast(F32)
+            for i in range(2 * pairs):
+                x_words[2 * q + i] = words[:, 512 * i : 512 * i + 512]
 
-        def copy_words(xt, dst_bf16, eng):
+        wa_words = []
+        for u in range(2):
+            wa_raw = const.tile([P, 2 * C], BF16, name="wa_raw%d" % u)
+            nc.sync.dma_start(
+                out=wa_raw[:].rearrange("p (s k) -> p s k", s=2), in_=wa_rows[:, 2 * u : 2 * u + 2, :]
+            )
+            wa_words.append(wa_raw[:].bitcast(F32))
+            if u == 0:
+                load_x(0, 1)
+        nc.scalar.dma_start(out=g_row[0:1, :], in_=kva_norm_w.rearrange("(o k) -> o k", o=1))
+        wr_raw = const.tile([P, C], BF16, name="wr_raw")
+        nc.sync.dma_start(out=wr_raw[:], in_=w_kva[KVL : KVL + R, :])
+        load_x(1, 1)
+        load_x(2, 1)
+        wb_raw = const.tile([P, 8 * KVL], BF16, name="wb_raw")
+        nc.sync.dma_start(
+            out=wb_raw[:].rearrange("p (r k) -> p r k", r=8), in_=w_kvb.rearrange("(r p) k -> p r k", p=P)
+        )
+        load_x(3, 1)
+        for q in range(4, N_PAIRS, 2):
+            load_x(q, 2)
+
+        tab = const.tile([P, TPP, 3, 64], F32, name="tab")
+        turns = const.tile([P, TPP, 64], F32, name="turns")
+        nc.vector.tensor_scalar(
+            out=turns[:, :, 0], in0=pos_i[:], scalar1=1.0 / (2.0 * math.pi), scalar2=None, op0=ALU.mult
+        )
+        for s in range(6):
+            n = 2**s
+            nc.vector.tensor_scalar(
+                out=turns[:, :, n : 2 * n], in0=turns[:, :, 0:n], scalar1=RATIO**n, scalar2=None, op0=ALU.mult
+            )
+        whole = const.tile([P, TPP, 64], I32, name="whole")
+        nc.vector.tensor_copy(out=whole[:], in_=turns[:])
+        frac = const.tile([P, TPP, 64], F32, name="frac")
+        nc.vector.tensor_tensor(out=frac[:], in0=turns[:], in1=whole[:], op=ALU.subtract)
+        sin_h = const.tile([P, TPP, 64], F32, name="sin_h")
+        nc.scalar.activation(out=sin_h[:], in_=frac[:], func=ACT.Sin, scale=math.pi)
+        nc.scalar.activation(out=tab[:, :, 2, :], in_=frac[:], func=ACT.Sin, scale=2.0 * math.pi)
+        sq_h = const.tile([P, TPP, 64], F32, name="sq_h")
+        nc.gpsimd.tensor_tensor(out=sq_h[:], in0=sin_h[:], in1=sin_h[:], op=ALU.mult)
+        nc.gpsimd.tensor_scalar(
+            out=tab[:, :, 1, :], in0=sq_h[:], scalar1=-2.0, scalar2=1.0, op0=ALU.mult, op1=ALU.add
+        )
+        nc.gpsimd.tensor_scalar(
+            out=tab[:, :, 0, :], in0=tab[:, :, 2, :], scalar1=-1.0, scalar2=0.0, op0=ALU.mult, op1=ALU.add
+        )
+
+        wl_q = const.tile([P, 2 * KVL], U32, name="wl_q", align_bytes=64)
+        wl_s = const.tile([P, 2 * KVL], U8, name="wl_s", align_bytes=64)
+        wr_q = const.tile([P, 2 * R], U32, name="wr_q", align_bytes=64)
+        wr_s = const.tile([P, 2 * R], U8, name="wr_s", align_bytes=64)
+        wb_q = const.tile([P, 1024], U32, name="wb_q", align_bytes=64)
+        wb_s = const.tile([P, 1024], U8, name="wb_s", align_bytes=64)
+        g_bc = const.tile([P, KVL], BF16, name="g_bc")
+
+        def transposes(blocks, name, tag):
+            ps = bank([P, 512], name, tag)
+            for i, words in enumerate(blocks):
+                nc.tensor.transpose(out=ps[:, P * i : P * i + P], in_=words, identity=ident[:])
+            return ps
+
+        def every_2nd(words, at):
+            return [words[:, at + v : at + 256 : 2] for v in range(2)]
+
+        def interleave(ps, dst, eng):
             engines[eng](
-                out=dst_bf16.bitcast(F32).rearrange("p (g w u) -> p g w u", g=2, u=2),
-                in_=xt[:].rearrange("p (g u w) -> p g w u", g=2, u=2),
+                out=dst.bitcast(F32).rearrange("p (g w v) -> p g w v", g=2, v=2),
+                in_=ps[:].rearrange("p (g v w) -> p g w v", g=2, v=2),
             )
 
-        with tc.tile_pool(name="setup", bufs=1) as setup:
-            g_row = setup.tile([P, KVL], BF16, name="g_row")
-            nc.vector.memset(g_row[:], 0.0)
-            nc.scalar.dma_start(out=g_row[0:1, :], in_=kva_norm_w.rearrange("(o k) -> o k", o=1))
-            ones = setup.tile([P, P], BF16, name="ones")
-            nc.vector.memset(ones[:], 1.0)
-            war = setup.tile([P, 5 * C], BF16, name="war")
-            nc.sync.dma_start(
-                out=war[:, 0 : 4 * C].rearrange("p (t k) -> p t k", t=4),
-                in_=w_kva[0:KVL, :].rearrange("(p t) k -> p t k", t=4),
-            )
-            nc.sync.dma_start(out=war[:, 4 * C : 5 * C], in_=w_kva[KVL : KVL + R, :])
-            wbr = setup.tile([P, 8 * KVL], BF16, name="wbr")
-            nc.sync.dma_start(
-                out=wbr[:].rearrange("p (r k) -> p r k", r=8), in_=w_kvb.rearrange("(r p) k -> p r k", p=P)
-            )
-            for hb in range(8):
-                xr = xin.tile([P, 4 * C], BF16, name="xr", tag="xr")
-                nc.sync.dma_start(out=xr[:], in_=x_rows[hb // 2][:, 4 * C * (hb % 2) : 4 * C * (hb % 2) + 4 * C])
-                x_words.append(xr[:].bitcast(F32))
+        def quantise(codes, scales, src):
+            nc.vector.quantize_mx(out=codes.bitcast(FP8X4), scales=scales, in_=src)
 
-            pos_i = setup.tile([P, TPP], I32, name="pos_i")
-            nc.gpsimd.iota(pos_i[:], pattern=[[1, TPP]], base=0, channel_multiplier=TPP)
-            make_identity(nc, ident_f[:])
-            make_identity(nc, ident_b[:])
-            nc.vector.memset(eps_t[:], EPS)
-            pos_f = setup.tile([P, TPP], F32, name="pos_f")
-            nc.vector.tensor_copy(out=pos_f[:], in_=pos_i[:])
-            inv = setup.tile([P, 64], F32, name="inv")
-            nc.vector.memset(inv[:, 0:1], 1.0)
-            for s in range(6):
-                n = 2**s
-                nc.vector.tensor_scalar(
-                    out=inv[:, n : 2 * n], in0=inv[:, 0:n], scalar1=RATIO**n, scalar2=None, op0=ALU.mult
-                )
-            turns = setup.tile([P, TPP, 64], F32, name="turns")
-            nc.vector.scalar_tensor_tensor(
-                out=turns[:],
-                in0=pos_f[:].unsqueeze(2).to_broadcast([P, TPP, 64]),
-                scalar=1.0 / (2.0 * math.pi),
-                in1=inv[:].unsqueeze(1).to_broadcast([P, TPP, 64]),
-                op0=ALU.mult,
-                op1=ALU.mult,
+        def wa_transpose(u, g, tag):
+            return transposes(
+                every_2nd(wa_words[u], 256 * g) + every_2nd(wa_words[u], 512 + 256 * g), "wa_ps", tag
             )
-            whole_i = setup.tile([P, TPP, 64], I32, name="whole_i")
-            nc.vector.tensor_copy(out=whole_i[:], in_=turns[:])
-            whole_f = setup.tile([P, TPP, 64], F32, name="whole_f")
-            nc.vector.tensor_copy(out=whole_f[:], in_=whole_i[:])
-            frac = setup.tile([P, TPP, 64], F32, name="frac")
-            nc.vector.tensor_tensor(out=frac[:], in0=turns[:], in1=whole_f[:], op=ALU.subtract)
-            nc.scalar.activation(out=sin_h[:], in_=frac[:], func=ACT.Sin, scale=math.pi)
-            nc.scalar.activation(out=sin_q[:], in_=frac[:], func=ACT.Sin, scale=0.5 * math.pi)
 
-            war_w = war[:].bitcast(F32)
-            for r in range(5):
-                xt = transpose_words(war_w[:, 512 * r : 512 * r + 512])
-                grp = stage.tile([P, 1024], BF16, name="grp", tag="cgrp", align_bytes=64)
-                copy_words(xt, grp[:], "SV"[r % 2])
-                for g in range(2):
-                    cols = slice(640 * g + P * r, 640 * g + P * r + P)
-                    nc.vector.quantize_mx(
-                        out=waq[:, cols].bitcast(FP8X4), scales=was[:, cols], in_=grp[:, 512 * g : 512 * g + 512]
-                    )
-            wbr_w = wbr[:].bitcast(F32)
-            for n, (ra, rb, dest) in enumerate(((0, 2, 0), (4, 6, 256), (1, 3, 512), (5, 7, 768))):
-                wt = k_bank([P, 512], F32, "wt")
-                for a, r in enumerate((ra, rb)):
-                    for u in range(2):
-                        nc.tensor.transpose(
-                            out=wt[:, 256 * a + P * u : 256 * a + P * u + P],
-                            in_=wbr_w[:, 256 * r + u : 256 * r + 256 : 2],
-                            identity=ident_f[:],
-                        )
-                grp = stage.tile([P, 1024], BF16, name="grp", tag="cgrp", align_bytes=64)
-                copy_words(wt, grp[:], "VS"[n % 2])
-                nc.vector.quantize_mx(
-                    out=wbq[:, dest : dest + 256].bitcast(FP8X4), scales=wbs[:, dest : dest + 256], in_=grp[:]
-                )
+        def wa_copy(ps, eng):
+            grp = stage.tile([P, 1024], BF16, name="wgrp", tag="wgrp", align_bytes=64)
+            engines[eng](
+                out=grp[:].bitcast(F32).rearrange("p (m e v) -> p m e v", e=2, v=2),
+                in_=ps[:].rearrange("p (e v m) -> p m e v", e=2, v=2),
+            )
+            return grp
 
-            g_ps = k_bank([P, KVL], F32, "g_ps")
+        def wa_quantise(u, g, grp):
+            cols = slice(KVL * g + 256 * u, KVL * g + 256 * u + 256)
+            quantise(wl_q[:, cols], wl_s[:, cols], grp[:])
+
+        def wr_prepare(tag, eng):
+            words = wr_raw[:].bitcast(F32)
+            ps = transposes(every_2nd(words, 0) + every_2nd(words, 256), "wr_ps", tag)
+            grp = stage.tile([P, 1024], BF16, name="wgrp", tag="wgrp", align_bytes=64)
+            interleave(ps, grp[:], eng)
+            quantise(wr_q[:], wr_s[:], grp[:])
+
+        def wb_prepare(i, tag, eng):
+            words = wb_raw[:].bitcast(F32)
+            ra, rb = ((0, 2), (4, 6), (1, 3), (5, 7))[i]
+            ps = transposes(every_2nd(words, 256 * ra) + every_2nd(words, 256 * rb), "wb_ps", tag)
+            grp = stage.tile([P, 1024], BF16, name="wgrp", tag="wgrp", align_bytes=64)
+            interleave(ps, grp[:], eng)
+            cols = slice(256 * i, 256 * i + 256)
+            quantise(wb_q[:, cols], wb_s[:, cols], grp[:])
+
+        def gain():
+            g_ps = bank([P, KVL], "g_ps", "K2")
             nc.tensor.matmul(out=g_ps[:], lhsT=ones[:], rhs=g_row[:], start=True, stop=True)
             nc.scalar.copy(
-                out=g_bc[:].rearrange("p (t m) -> p t m", t=4), in_=g_ps[:].rearrange("p (m t) -> p t m", t=4)
-            )
-
-        def finish_tables():
-            nc.scalar.activation(out=sq_q[:], in_=sin_q[:], func=ACT.Square)
-            nc.scalar.activation(out=cos_h[:], in_=sq_q[:], func=ACT.Copy, scale=-2.0, bias=1.0)
-            nc.scalar.activation(out=sq_h[:], in_=sin_h[:], func=ACT.Square)
-            nc.scalar.activation(out=tab1[:, :, 0, :], in_=sq_h[:], func=ACT.Copy, scale=-2.0, bias=1.0)
-            nc.scalar.activation(out=tab2[:, :, 1, :], in_=sq_h[:], func=ACT.Copy, scale=-2.0, bias=1.0)
-            nc.vector.scalar_tensor_tensor(
-                out=tab1[:, :, 1, :], in0=sin_h[:], scalar=2.0, in1=cos_h[:], op0=ALU.mult, op1=ALU.mult
-            )
-            nc.vector.scalar_tensor_tensor(
-                out=tab2[:, :, 0, :], in0=sin_h[:], scalar=-2.0, in1=cos_h[:], op0=ALU.mult, op1=ALU.mult
+                out=g_bc[:].rearrange("p (u m e) -> p u m e", u=2, e=2),
+                in_=g_ps[:].rearrange("p (m u e) -> p u m e", u=2, e=2),
             )
 
         def x_transpose(q):
             live["xt", q] = [
-                transpose_words(x_words[(2 * q + a) // 4][:, 512 * ((2 * q + a) % 4) : 512 * ((2 * q + a) % 4) + 512])
+                transposes(every_2nd(x_words[2 * q + a], 0) + every_2nd(x_words[2 * q + a], 256), "xt", "X%d" % a)
                 for a in range(2)
             ]
 
         def x_copy(q):
             xg = stage.tile([P, 2048], BF16, name="xg", tag="xgrp", align_bytes=64)
             for a in range(2):
-                copy_words(live["xt", q][a], xg[:, 1024 * a : 1024 * a + 1024], "SV"[a])
+                interleave(live["xt", q][a], xg[:, 1024 * a : 1024 * a + 1024], "S")
             live["xg", q] = xg
 
         def x_quantise(q):
             xq = ring.tile([P, 512], U32, name="xq", tag="xq", align_bytes=64)
             xs = ring.tile([P, 512], U8, name="xs", tag="xs", align_bytes=64)
-            nc.vector.quantize_mx(out=xq[:].bitcast(FP8X4), scales=xs[:], in_=live["xg", q][:])
+            quantise(xq[:], xs[:], live["xg", q][:])
             live["xq", q] = (xq, xs)
 
-        def stage1_pass(out, q, a, g, lo, hi):
+        def stage1_pass(out, q, a, g, codes, scales):
             xq, xs = live["xq", q]
             xc = slice(256 * a + P * g, 256 * a + P * g + P)
             nc.tensor.matmul_mx(
                 out=out,
                 lhsT=xq[:, xc].bitcast(FP8X4),
                 lhsT_scale=xs[:, xc],
-                rhs=waq[:, 640 * g + lo : 640 * g + hi].bitcast(FP8X4),
-                rhs_scale=was[:, 640 * g + lo : 640 * g + hi],
+                rhs=codes.bitcast(FP8X4),
+                rhs_scale=scales,
                 start=(g == 0),
                 stop=(g == 1),
             )
 
-        def stage1_latent(q):
-            tiles = []
-            for a in range(2):
-                l = psum.tile([P, KVL], F32, name="l", tag="L%d" % a)
-                for g in range(2):
-                    stage1_pass(l[:], q, a, g, 0, KVL)
-                tiles.append(l)
-            live["l", q] = tiles
+        def stage1_latent(q, a):
+            l = bank([P, KVL], "l", "L%d" % a)
+            for g in range(2):
+                cols = slice(KVL * g, KVL * g + KVL)
+                stage1_pass(l[:], q, a, g, wl_q[:, cols], wl_s[:, cols])
+            live["l", q, a] = l
 
         def stage1_rotary(q):
-            r_ps = psum.tile([P, 2, R], F32, name="r_ps", tag="R")
+            r_ps = bank([P, 2, R], "r_ps", "RC")
             for a in range(2):
                 for g in range(2):
-                    stage1_pass(r_ps[:, a, :], q, a, g, KVL, KVL + R)
+                    cols = slice(R * g, R * g + R)
+                    stage1_pass(r_ps[:, a, :], q, a, g, wr_q[:, cols], wr_s[:, cols])
             live["r", q] = r_ps
 
         def squares(q):
             ssq = small.tile([P, 2], F32, name="ssq", tag="ssq")
             for a in range(2):
-                junk = work.tile([P, KVL], BF16, name="junk", tag="junk", bufs=2)
-                nc.scalar.activation(out=junk[:], in_=live["l", q][a][:], func=ACT.Square, accum_out=ssq[:, a : a + 1])
+                junk = work.tile([P, KVL], BF16, name="junk", tag="junk")
+                nc.scalar.activation(
+                    out=junk[:], in_=live["l", q, a][:], func=ACT.Square, accum_out=ssq[:, a : a + 1]
+                )
             rstd = small.tile([P, 2], F32, name="rstd", tag="rstd")
             nc.scalar.activation(
                 out=rstd[:], in_=ssq[:], func=ACT.Abs_reciprocal_sqrt, scale=1.0 / KVL, bias=eps_t[:, 0:1]
@@ -235,13 +235,12 @@ def tile_multiheadlatentattention_pb_t_kernel(tc, x, w_kva, kva_norm_w, w_kvb, o
             live["rstd", q] = rstd
 
         def normalise(q):
-            rstd = live["rstd", q]
             c_sb = work.tile([P, 2, KVL], BF16, name="c_sb", tag="c_sb")
             for a in range(2):
                 nc.vector.scalar_tensor_tensor(
                     out=c_sb[:, a, :],
-                    in0=live["l", q][a][:],
-                    scalar=rstd[:, a : a + 1],
+                    in0=live["l", q, a][:],
+                    scalar=live["rstd", q][:, a : a + 1],
                     in1=g_bc[:],
                     op0=ALU.mult,
                     op1=ALU.mult,
@@ -249,132 +248,139 @@ def tile_multiheadlatentattention_pb_t_kernel(tc, x, w_kva, kva_norm_w, w_kvb, o
             live["c", q] = c_sb
 
         def c_transpose(q):
-            ct = psum.tile([P, 2, 4, P], BF16, name="ct", tag="C")
-            for a in range(2):
-                for j in range(4):
-                    nc.tensor.transpose(
-                        out=ct[:, a, j, :], in_=live["c", q][:, a, P * j : P * j + P], identity=ident_b[:]
-                    )
-            live["ct", q] = ct
+            words = [live["c", q][:, a, :].bitcast(F32) for a in range(2)]
+            live["ct", q] = transposes([words[a][:, P * v : P * v + P] for a in range(2) for v in range(2)], "ct", "RC")
 
         def c_copy(q):
-            grp = stage.tile([P, 1024], BF16, name="grp", tag="cgrp", align_bytes=64)
-            nc.scalar.copy(
-                out=grp[:].rearrange("p (a w j) -> p a w j", a=2, j=4),
-                in_=live["ct", q][:].rearrange("p a j w -> p a w j"),
-            )
+            grp = stage.tile([P, 1024], BF16, name="cgrp", tag="cgrp", align_bytes=64)
+            interleave(live["ct", q], grp[:], "S")
             live["cg", q] = grp
 
         def c_quantise(q):
             cq = work.tile([P, 256], U32, name="cq", tag="cq", align_bytes=64)
             cs = work.tile([P, 256], U8, name="cs", tag="cs", align_bytes=64)
-            nc.vector.quantize_mx(out=cq[:].bitcast(FP8X4), scales=cs[:], in_=live["cg", q][:])
+            quantise(cq[:], cs[:], live["cg", q][:])
             live["cq", q] = (cq, cs)
 
-        def stage2(q):
+        def stage2(q, i):
             cq, cs = live["cq", q]
-            banks = []
-            for a in range(2):
-                for part in range(2):
-                    kv = k_bank([P, 512], F32, "kv")
-                    nc.tensor.matmul_mx(
-                        out=kv[:],
-                        lhsT=cq[:, P * a : P * a + P].bitcast(FP8X4),
-                        lhsT_scale=cs[:, P * a : P * a + P],
-                        rhs=wbq[:, 512 * part : 512 * part + 512].bitcast(FP8X4),
-                        rhs_scale=wbs[:, 512 * part : 512 * part + 512],
-                        start=True,
-                        stop=True,
-                    )
-                    banks.append(kv)
-            live["kv", q] = banks
+            a, part = i // 2, i % 2
+            kv = bank([P, 512], "kv", "K%d" % (i % 3))
+            nc.tensor.matmul_mx(
+                out=kv[:],
+                lhsT=cq[:, P * a : P * a + P].bitcast(FP8X4),
+                lhsT_scale=cs[:, P * a : P * a + P],
+                rhs=wb_q[:, 512 * part : 512 * part + 512].bitcast(FP8X4),
+                rhs_scale=wb_s[:, 512 * part : 512 * part + 512],
+                start=True,
+                stop=True,
+            )
+            live["kv", q, i] = kv
 
-        with tc.tile_pool(name="outp", bufs=6) as outp:
-
-            def rotate(q):
-                t0 = 2 * (q % 4)
-                k_sb = outp.tile([P, 2, H, 256], F32, name="k_sb", tag="k_sb")
-                v_sb = outp.tile([P, 2, H * 128], F32, name="v_sb", tag="v_sb")
-                live["out", q] = (k_sb, v_sb)
-                r_pairs = live["r", q][:].rearrange("p t (j e) -> p t e j", e=2)
-                m1 = work.tile([P, 2, 2, 64], F32, name="m1", tag="m1")
+        def rotate(q):
+            t0 = 2 * (q % 4)
+            k_sb = outp.tile([P, 2, H, 256], F32, name="k_sb", tag="k_sb")
+            v_sb = outp.tile([P, 2, H * 128], F32, name="v_sb", tag="v_sb")
+            live["out", q] = (k_sb, v_sb)
+            r_pairs = live["r", q][:].rearrange("p t (j e) -> p t e j", e=2)
+            products = []
+            for e in range(2):
+                m = work.tile([P, 2, 2, 64], F32, name="m", tag="m%d" % e)
                 nc.vector.tensor_tensor(
-                    out=m1[:],
-                    in0=r_pairs[:, :, 0:1, :].to_broadcast([P, 2, 2, 64]),
-                    in1=tab1[:, t0 : t0 + 2, :, :],
+                    out=m[:],
+                    in0=r_pairs[:, :, e : e + 1, :].to_broadcast([P, 2, 2, 64]),
+                    in1=tab[:, t0 : t0 + 2, 1 - e : 3 - e, :],
                     op=ALU.mult,
                 )
-                m2 = work.tile([P, 2, 2, 64], F32, name="m2", tag="m2")
-                nc.vector.tensor_tensor(
-                    out=m2[:],
-                    in0=r_pairs[:, :, 1:2, :].to_broadcast([P, 2, 2, 64]),
-                    in1=tab2[:, t0 : t0 + 2, :, :],
-                    op=ALU.mult,
-                )
-                nc.gpsimd.tensor_tensor(
-                    out=k_sb[:, :, 0, 128:256].rearrange("p t (j e) -> p t j e", e=2),
-                    in0=m1[:].rearrange("p t e j -> p t j e"),
-                    in1=m2[:].rearrange("p t e j -> p t j e"),
-                    op=ALU.add,
-                )
-                nc.gpsimd.tensor_scalar(
-                    out=k_sb[:, :, 1:4, 128:256],
-                    in0=k_sb[:, :, 0:1, 128:256].to_broadcast([P, 2, 3, 128]),
-                    scalar1=1.0,
-                    scalar2=0.0,
-                    op0=ALU.mult,
-                    op1=ALU.add,
-                )
+                products.append(m)
+            nc.gpsimd.tensor_tensor(
+                out=k_sb[:, :, 0, 128:256].rearrange("p t (j e) -> p t j e", e=2),
+                in0=products[0][:].rearrange("p t e j -> p t j e"),
+                in1=products[1][:].rearrange("p t e j -> p t j e"),
+                op=ALU.add,
+            )
+            nc.gpsimd.tensor_scalar(
+                out=k_sb[:, :, 1:4, 128:256],
+                in0=k_sb[:, :, 0:1, 128:256].to_broadcast([P, 2, 3, 128]),
+                scalar1=1.0,
+                scalar2=0.0,
+                op0=ALU.mult,
+                op1=ALU.add,
+            )
 
-            def copy_out(q):
-                k_sb, v_sb = live["out", q]
-                for a in range(2):
-                    eng = engines["SV"[a]]
-                    eng(out=k_sb[:, a, :, 0:128], in_=live["kv", q][2 * a][:].rearrange("p (h d) -> p h d", h=H))
-                    eng(out=v_sb[:, a, :], in_=live["kv", q][2 * a + 1][:])
+        def copy_out(q, i, eng):
+            k_sb, v_sb = live["out", q]
+            a, part = i // 2, i % 2
+            kv = live["kv", q, i]
+            if part == 0:
+                engines[eng](out=k_sb[:, a, :, 0:128], in_=kv[:].rearrange("p (h d) -> p h d", h=H))
+            else:
+                engines[eng](out=v_sb[:, a, :], in_=kv[:])
 
-            def store(q):
-                k_sb, v_sb = live["out", q]
-                b = q // 4
-                t0 = 2 * (q % 4)
-                nc.sync.dma_start(out=k_rows[b][:, t0 : t0 + 2, :], in_=k_sb[:].rearrange("p t h d -> p t (h d)"))
-                nc.sync.dma_start(out=v_rows[b][:, t0 : t0 + 2, :], in_=v_sb[:])
+        def store(q):
+            k_sb, v_sb = live["out", q]
+            b = q // 4
+            t0 = 2 * (q % 4)
+            nc.sync.dma_start(out=k_rows[b][:, t0 : t0 + 2, :], in_=k_sb[:].rearrange("p t h d -> p t (h d)"))
+            nc.sync.dma_start(out=v_rows[b][:, t0 : t0 + 2, :], in_=v_sb[:])
 
-            def is_pair(q):
-                return 0 <= q < N_PAIRS
+        def is_pair(q):
+            return 0 <= q < N_PAIRS
 
-            x_transpose(0)
-            x_copy(0)
-            x_quantise(0)
-            next_x = 1
-            for n in range(N_PAIRS + 3):
-                fresh = [q for q in range(next_x, next_x + (2 if n < 3 else 1)) if is_pair(q)]
-                next_x = next_x + len(fresh)
-                for q in fresh:
-                    x_transpose(q)
-                if is_pair(n - 2):
-                    c_transpose(n - 2)
-                if is_pair(n - 1):
-                    squares(n - 1)
-                for q in fresh:
-                    x_copy(q)
-                if is_pair(n - 1):
-                    normalise(n - 1)
-                if is_pair(n - 2):
-                    c_copy(n - 2)
-                    c_quantise(n - 2)
-                for q in fresh:
-                    x_quantise(q)
-                if n == 0:
-                    finish_tables()
-                if is_pair(n - 3):
-                    stage2(n - 3)
-                if is_pair(n - 1):
-                    stage1_rotary(n - 1)
-                if is_pair(n):
-                    stage1_latent(n)
-                if is_pair(n - 1):
-                    rotate(n - 1)
-                if is_pair(n - 3):
-                    copy_out(n - 3)
-                    store(n - 3)
+        wa0 = [wa_transpose(0, g, "K%d" % g) for g in range(2)]
+        x_transpose(0)
+        grp0 = [wa_copy(wa0[g], "V") for g in range(2)]
+        for g in range(2):
+            wa_quantise(0, g, grp0[g])
+        x_copy(0)
+        wa1 = [wa_transpose(1, g, "K%d" % g) for g in range(2)]
+        x_quantise(0)
+        grp1 = [wa_copy(wa1[g], "SV"[g]) for g in range(2)]
+        for g in range(2):
+            wa_quantise(1, g, grp1[g])
+        warm = const.tile([P, 1], F32, name="warm")
+        nc.scalar.activation(out=warm[:], in_=eps_t[:], func=ACT.Abs_reciprocal_sqrt)
+        wr_prepare("K2", "V")
+
+        for n in range(N_PAIRS + 3):
+            if is_pair(n + 1):
+                x_transpose(n + 1)
+            if is_pair(n - 2):
+                c_transpose(n - 2)
+            if is_pair(n - 1):
+                normalise(n - 1)
+            if is_pair(n + 1):
+                x_copy(n + 1)
+            if is_pair(n - 2):
+                c_copy(n - 2)
+                c_quantise(n - 2)
+            if is_pair(n + 1):
+                x_quantise(n + 1)
+            if is_pair(n - 3):
+                for i in range(3):
+                    stage2(n - 3, i)
+                copy_out(n - 3, 0, "S")
+            if is_pair(n):
+                stage1_latent(n, 0)
+                stage1_latent(n, 1)
+                stage1_rotary(n)
+            if is_pair(n - 3):
+                stage2(n - 3, 3)
+                copy_out(n - 3, 1, "V")
+            if is_pair(n):
+                rotate(n)
+            if is_pair(n - 3):
+                copy_out(n - 3, 2, "V")
+            if is_pair(n):
+                squares(n)
+            if n == 0:
+                gain()
+                wb_prepare(0, "K0", "V")
+                wb_prepare(2, "K1", "S")
+            if n == 1:
+                wb_prepare(1, "K0", "V")
+                wb_prepare(3, "K1", "S")
+            if is_pair(n - 3):
+                copy_out(n - 3, 3, "S")
+            if is_pair(n - 3):
+                store(n - 3)

@@ -33,13 +33,18 @@ def tile_multiheadlatentattention_pb_t_kernel(tc, x, w_kva, kva_norm_w, w_kvb, o
         engines = {"S": nc.scalar.copy, "V": nc.vector.tensor_copy}
         live = {}
 
-        def bank(shape, name, tag):
+        state = {"g": 0}
+
+        def bank(shape, name, tag="G"):
+            if tag == "G":
+                tag = "G%d" % (state["g"] % 5)
+                state["g"] = state["g"] + 1
             return psum.tile(shape, F32, name=name, tag=tag)
 
         pos_i = const.tile([P, TPP], I32, name="pos_i")
         nc.gpsimd.iota(pos_i[:], pattern=[[1, TPP]], base=0, channel_multiplier=TPP)
         g_row = const.tile([P, KVL], BF16, name="g_row")
-        nc.gpsimd.memset(g_row[:], 0.0)
+        nc.vector.memset(g_row[:], 0.0)
         ident = const.tile([P, P], F32, name="ident")
         make_identity(nc, ident[:])
         ones = const.tile([P, P], BF16, name="ones")
@@ -73,11 +78,11 @@ def tile_multiheadlatentattention_pb_t_kernel(tc, x, w_kva, kva_norm_w, w_kvb, o
         wr_raw = const.tile([P, C], BF16, name="wr_raw")
         nc.sync.dma_start(out=wr_raw[:], in_=w_kva[KVL : KVL + R, :])
         load_x(1, 1)
-        load_x(2, 1)
         wb_raw = const.tile([P, 8 * KVL], BF16, name="wb_raw")
         nc.sync.dma_start(
             out=wb_raw[:].rearrange("p (r k) -> p r k", r=8), in_=w_kvb.rearrange("(r p) k -> p r k", p=P)
         )
+        load_x(2, 1)
         load_x(3, 1)
         for q in range(4, N_PAIRS, 2):
             load_x(q, 2)
@@ -99,14 +104,14 @@ def tile_multiheadlatentattention_pb_t_kernel(tc, x, w_kva, kva_norm_w, w_kvb, o
         sin_h = const.tile([P, TPP, 64], F32, name="sin_h")
         nc.scalar.activation(out=sin_h[:], in_=frac[:], func=ACT.Sin, scale=math.pi)
         nc.scalar.activation(out=tab[:, :, 2, :], in_=frac[:], func=ACT.Sin, scale=2.0 * math.pi)
+        nc.scalar.activation(out=tab[:, :, 0, :], in_=frac[:], func=ACT.Sin, scale=-2.0 * math.pi)
         sq_h = const.tile([P, TPP, 64], F32, name="sq_h")
-        nc.gpsimd.tensor_tensor(out=sq_h[:], in0=sin_h[:], in1=sin_h[:], op=ALU.mult)
-        nc.gpsimd.tensor_scalar(
-            out=tab[:, :, 1, :], in0=sq_h[:], scalar1=-2.0, scalar2=1.0, op0=ALU.mult, op1=ALU.add
-        )
-        nc.gpsimd.tensor_scalar(
-            out=tab[:, :, 0, :], in0=tab[:, :, 2, :], scalar1=-1.0, scalar2=0.0, op0=ALU.mult, op1=ALU.add
-        )
+
+        def finish_tables():
+            nc.vector.scalar_tensor_tensor(
+                out=sq_h[:], in0=sin_h[:], scalar=-2.0, in1=sin_h[:], op0=ALU.mult, op1=ALU.mult
+            )
+            nc.vector.tensor_scalar(out=tab[:, :, 1, :], in0=sq_h[:], scalar1=1.0, scalar2=None, op0=ALU.add)
 
         wl_q = const.tile([P, 2 * KVL], U32, name="wl_q", align_bytes=64)
         wl_s = const.tile([P, 2 * KVL], U8, name="wl_s", align_bytes=64)
@@ -116,7 +121,7 @@ def tile_multiheadlatentattention_pb_t_kernel(tc, x, w_kva, kva_norm_w, w_kvb, o
         wb_s = const.tile([P, 1024], U8, name="wb_s", align_bytes=64)
         g_bc = const.tile([P, KVL], BF16, name="g_bc")
 
-        def transposes(blocks, name, tag):
+        def transposes(blocks, name, tag="G"):
             ps = bank([P, 512], name, tag)
             for i, words in enumerate(blocks):
                 nc.tensor.transpose(out=ps[:, P * i : P * i + P], in_=words, identity=ident[:])
@@ -134,9 +139,9 @@ def tile_multiheadlatentattention_pb_t_kernel(tc, x, w_kva, kva_norm_w, w_kvb, o
         def quantise(codes, scales, src):
             nc.vector.quantize_mx(out=codes.bitcast(FP8X4), scales=scales, in_=src)
 
-        def wa_transpose(u, g, tag):
+        def wa_transpose(u, g):
             return transposes(
-                every_2nd(wa_words[u], 256 * g) + every_2nd(wa_words[u], 512 + 256 * g), "wa_ps", tag
+                every_2nd(wa_words[u], 256 * g) + every_2nd(wa_words[u], 512 + 256 * g), "wa_ps"
             )
 
         def wa_copy(ps, eng):
@@ -151,24 +156,24 @@ def tile_multiheadlatentattention_pb_t_kernel(tc, x, w_kva, kva_norm_w, w_kvb, o
             cols = slice(KVL * g + 256 * u, KVL * g + 256 * u + 256)
             quantise(wl_q[:, cols], wl_s[:, cols], grp[:])
 
-        def wr_prepare(tag, eng):
+        def wr_prepare(eng):
             words = wr_raw[:].bitcast(F32)
-            ps = transposes(every_2nd(words, 0) + every_2nd(words, 256), "wr_ps", tag)
+            ps = transposes(every_2nd(words, 0) + every_2nd(words, 256), "wr_ps")
             grp = stage.tile([P, 1024], BF16, name="wgrp", tag="wgrp", align_bytes=64)
             interleave(ps, grp[:], eng)
             quantise(wr_q[:], wr_s[:], grp[:])
 
-        def wb_prepare(i, tag, eng):
+        def wb_prepare(i, eng):
             words = wb_raw[:].bitcast(F32)
             ra, rb = ((0, 2), (4, 6), (1, 3), (5, 7))[i]
-            ps = transposes(every_2nd(words, 256 * ra) + every_2nd(words, 256 * rb), "wb_ps", tag)
+            ps = transposes(every_2nd(words, 256 * ra) + every_2nd(words, 256 * rb), "wb_ps")
             grp = stage.tile([P, 1024], BF16, name="wgrp", tag="wgrp", align_bytes=64)
             interleave(ps, grp[:], eng)
             cols = slice(256 * i, 256 * i + 256)
             quantise(wb_q[:, cols], wb_s[:, cols], grp[:])
 
         def gain():
-            g_ps = bank([P, KVL], "g_ps", "K2")
+            g_ps = bank([P, KVL], "g_ps", "RC")
             nc.tensor.matmul(out=g_ps[:], lhsT=ones[:], rhs=g_row[:], start=True, stop=True)
             nc.scalar.copy(
                 out=g_bc[:].rearrange("p (u m e) -> p u m e", u=2, e=2),
@@ -177,15 +182,15 @@ def tile_multiheadlatentattention_pb_t_kernel(tc, x, w_kva, kva_norm_w, w_kvb, o
 
         def x_transpose(q):
             live["xt", q] = [
-                transposes(every_2nd(x_words[2 * q + a], 0) + every_2nd(x_words[2 * q + a], 256), "xt", "X%d" % a)
+                transposes(every_2nd(x_words[2 * q + a], 0) + every_2nd(x_words[2 * q + a], 256), "xt")
                 for a in range(2)
             ]
 
-        def x_copy(q):
-            xg = stage.tile([P, 2048], BF16, name="xg", tag="xgrp", align_bytes=64)
-            for a in range(2):
-                interleave(live["xt", q][a], xg[:, 1024 * a : 1024 * a + 1024], "S")
-            live["xg", q] = xg
+        def x_copy(q, a, eng):
+            if a == 0:
+                xg = stage.tile([P, 2048], BF16, name="xg", tag="xgrp", align_bytes=64)
+                live["xg", q] = xg
+            interleave(live["xt", q][a], live["xg", q][:, 1024 * a : 1024 * a + 1024], eng)
 
         def x_quantise(q):
             xq = ring.tile([P, 512], U32, name="xq", tag="xq", align_bytes=64)
@@ -223,59 +228,69 @@ def tile_multiheadlatentattention_pb_t_kernel(tc, x, w_kva, kva_norm_w, w_kvb, o
 
         def squares(q):
             ssq = small.tile([P, 2], F32, name="ssq", tag="ssq")
+            live["ssq", q] = ssq
             for a in range(2):
                 junk = work.tile([P, KVL], BF16, name="junk", tag="junk")
                 nc.scalar.activation(
                     out=junk[:], in_=live["l", q, a][:], func=ACT.Square, accum_out=ssq[:, a : a + 1]
                 )
+
+        def inverse_rms(q):
+            ssq = live["ssq", q]
             rstd = small.tile([P, 2], F32, name="rstd", tag="rstd")
             nc.scalar.activation(
                 out=rstd[:], in_=ssq[:], func=ACT.Abs_reciprocal_sqrt, scale=1.0 / KVL, bias=eps_t[:, 0:1]
             )
             live["rstd", q] = rstd
 
-        def normalise(q):
-            c_sb = work.tile([P, 2, KVL], BF16, name="c_sb", tag="c_sb")
-            for a in range(2):
-                nc.vector.scalar_tensor_tensor(
-                    out=c_sb[:, a, :],
-                    in0=live["l", q, a][:],
-                    scalar=live["rstd", q][:, a : a + 1],
-                    in1=g_bc[:],
-                    op0=ALU.mult,
-                    op1=ALU.mult,
-                )
-            live["c", q] = c_sb
+        def normalise(q, a):
+            c_sb = work.tile([P, KVL], BF16, name="c_sb", tag="c_sb", bufs=6)
+            nc.vector.scalar_tensor_tensor(
+                out=c_sb[:],
+                in0=live["l", q, a][:],
+                scalar=live["rstd", q][:, a : a + 1],
+                in1=g_bc[:],
+                op0=ALU.mult,
+                op1=ALU.mult,
+            )
+            live["c", 2 * q + a] = c_sb
 
-        def c_transpose(q):
-            words = [live["c", q][:, a, :].bitcast(F32) for a in range(2)]
-            live["ct", q] = transposes([words[a][:, P * v : P * v + P] for a in range(2) for v in range(2)], "ct", "RC")
+        def c_transpose(tiles):
+            blocks = []
+            for t in tiles:
+                words = live["c", t][:].bitcast(F32)
+                blocks = blocks + [words[:, P * v : P * v + P] for v in range(2)]
+            live["ct", tiles] = transposes(blocks, "ct", "RC")
 
-        def c_copy(q):
+        def c_copy(tiles, eng):
+            w = len(tiles)
             grp = stage.tile([P, 1024], BF16, name="cgrp", tag="cgrp", align_bytes=64)
-            interleave(live["ct", q], grp[:], "S")
-            live["cg", q] = grp
+            engines[eng](
+                out=grp[:, 0 : 512 * w].bitcast(F32).rearrange("p (g w v) -> p g w v", g=w, v=2),
+                in_=live["ct", tiles][:, 0 : 256 * w].rearrange("p (g v w) -> p g w v", g=w, v=2),
+            )
+            live["cg", tiles] = grp
 
-        def c_quantise(q):
+        def c_quantise(tiles):
+            w = len(tiles)
             cq = work.tile([P, 256], U32, name="cq", tag="cq", align_bytes=64)
             cs = work.tile([P, 256], U8, name="cs", tag="cs", align_bytes=64)
-            quantise(cq[:], cs[:], live["cg", q][:])
-            live["cq", q] = (cq, cs)
+            quantise(cq[:, 0 : P * w], cs[:, 0 : P * w], live["cg", tiles][:, 0 : 512 * w])
+            live["cq", tiles] = (cq, cs)
 
-        def stage2(q, i):
-            cq, cs = live["cq", q]
-            a, part = i // 2, i % 2
-            kv = bank([P, 512], "kv", "K%d" % (i % 3))
+        def stage2(tiles, i, part):
+            cq, cs = live["cq", tiles]
+            kv = bank([P, 512], "kv")
             nc.tensor.matmul_mx(
                 out=kv[:],
-                lhsT=cq[:, P * a : P * a + P].bitcast(FP8X4),
-                lhsT_scale=cs[:, P * a : P * a + P],
+                lhsT=cq[:, P * i : P * i + P].bitcast(FP8X4),
+                lhsT_scale=cs[:, P * i : P * i + P],
                 rhs=wb_q[:, 512 * part : 512 * part + 512].bitcast(FP8X4),
                 rhs_scale=wb_s[:, 512 * part : 512 * part + 512],
                 start=True,
                 stop=True,
             )
-            live["kv", q, i] = kv
+            live["kv", tiles[i], part] = kv
 
         def rotate(q):
             t0 = 2 * (q % 4)
@@ -293,94 +308,107 @@ def tile_multiheadlatentattention_pb_t_kernel(tc, x, w_kva, kva_norm_w, w_kvb, o
                     op=ALU.mult,
                 )
                 products.append(m)
-            nc.gpsimd.tensor_tensor(
+            live["m", q] = products
+
+        def rotate_add(q, eng):
+            k_sb = live["out", q][0]
+            products = live["m", q]
+            eng.tensor_tensor(
                 out=k_sb[:, :, 0, 128:256].rearrange("p t (j e) -> p t j e", e=2),
                 in0=products[0][:].rearrange("p t e j -> p t j e"),
                 in1=products[1][:].rearrange("p t e j -> p t j e"),
                 op=ALU.add,
             )
-            nc.gpsimd.tensor_scalar(
-                out=k_sb[:, :, 1:4, 128:256],
-                in0=k_sb[:, :, 0:1, 128:256].to_broadcast([P, 2, 3, 128]),
-                scalar1=1.0,
-                scalar2=0.0,
-                op0=ALU.mult,
-                op1=ALU.add,
-            )
 
-        def copy_out(q, i, eng):
-            k_sb, v_sb = live["out", q]
-            a, part = i // 2, i % 2
-            kv = live["kv", q, i]
+        def rotate_spread(q, heads):
+            k_sb = live["out", q][0]
+            for h0, h1 in heads:
+                nc.gpsimd.tensor_scalar(
+                    out=k_sb[:, :, h0:h1, 128:256],
+                    in0=k_sb[:, :, 0:1, 128:256].to_broadcast([P, 2, h1 - h0, 128]),
+                    scalar1=1.0,
+                    scalar2=0.0,
+                    op0=ALU.mult,
+                    op1=ALU.add,
+                )
+
+        def copy_out(t, part, eng):
+            k_sb, v_sb = live["out", t // 2]
+            a = t % 2
+            kv = live["kv", t, part]
             if part == 0:
                 engines[eng](out=k_sb[:, a, :, 0:128], in_=kv[:].rearrange("p (h d) -> p h d", h=H))
             else:
                 engines[eng](out=v_sb[:, a, :], in_=kv[:])
 
-        def store(q):
+        def store(q, lo, hi):
             k_sb, v_sb = live["out", q]
             b = q // 4
             t0 = 2 * (q % 4)
-            nc.sync.dma_start(out=k_rows[b][:, t0 : t0 + 2, :], in_=k_sb[:].rearrange("p t h d -> p t (h d)"))
-            nc.sync.dma_start(out=v_rows[b][:, t0 : t0 + 2, :], in_=v_sb[:])
+            nc.sync.dma_start(
+                out=k_rows[b][:, t0 + lo : t0 + hi, :], in_=k_sb[:, lo:hi].rearrange("p t h d -> p t (h d)")
+            )
+            nc.sync.dma_start(out=v_rows[b][:, t0 + lo : t0 + hi, :], in_=v_sb[:, lo:hi, :])
 
         def is_pair(q):
             return 0 <= q < N_PAIRS
 
-        wa0 = [wa_transpose(0, g, "K%d" % g) for g in range(2)]
+        wa0 = [wa_transpose(0, g) for g in range(2)]
         x_transpose(0)
         grp0 = [wa_copy(wa0[g], "V") for g in range(2)]
         for g in range(2):
             wa_quantise(0, g, grp0[g])
-        x_copy(0)
-        wa1 = [wa_transpose(1, g, "K%d" % g) for g in range(2)]
+        x_copy(0, 0, "S")
+        x_copy(0, 1, "S")
+        wa1 = [wa_transpose(1, g) for g in range(2)]
         x_quantise(0)
         grp1 = [wa_copy(wa1[g], "SV"[g]) for g in range(2)]
         for g in range(2):
             wa_quantise(1, g, grp1[g])
         warm = const.tile([P, 1], F32, name="warm")
         nc.scalar.activation(out=warm[:], in_=eps_t[:], func=ACT.Abs_reciprocal_sqrt)
-        wr_prepare("K2", "V")
+        wr_prepare("V")
 
-        for n in range(N_PAIRS + 3):
+        for n in range(N_PAIRS + 1):
+            last = (2 * n - 2, 2 * n - 1)
             if is_pair(n + 1):
                 x_transpose(n + 1)
-            if is_pair(n - 2):
-                c_transpose(n - 2)
             if is_pair(n - 1):
-                normalise(n - 1)
+                c_transpose(last)
             if is_pair(n + 1):
-                x_copy(n + 1)
-            if is_pair(n - 2):
-                c_copy(n - 2)
-                c_quantise(n - 2)
+                x_copy(n + 1, 0, "S")
+                x_copy(n + 1, 1, "S")
+            if is_pair(n - 1):
+                c_copy(last, "V")
+                c_quantise(last)
             if is_pair(n + 1):
                 x_quantise(n + 1)
-            if is_pair(n - 3):
-                for i in range(3):
-                    stage2(n - 3, i)
-                copy_out(n - 3, 0, "S")
             if is_pair(n):
                 stage1_latent(n, 0)
                 stage1_latent(n, 1)
                 stage1_rotary(n)
-            if is_pair(n - 3):
-                stage2(n - 3, 3)
-                copy_out(n - 3, 1, "V")
-            if is_pair(n):
-                rotate(n)
-            if is_pair(n - 3):
-                copy_out(n - 3, 2, "V")
-            if is_pair(n):
                 squares(n)
+                inverse_rms(n)
             if n == 0:
                 gain()
-                wb_prepare(0, "K0", "V")
-                wb_prepare(2, "K1", "S")
-            if n == 1:
-                wb_prepare(1, "K0", "V")
-                wb_prepare(3, "K1", "S")
-            if is_pair(n - 3):
-                copy_out(n - 3, 3, "S")
-            if is_pair(n - 3):
-                store(n - 3)
+                finish_tables()
+            if is_pair(n):
+                rotate(n)
+                rotate_add(n, nc.gpsimd)
+                rotate_spread(n, [(1, 4)])
+            if is_pair(n - 1):
+                for i in range(2):
+                    for part in range(2):
+                        stage2(last, i, part)
+            if is_pair(n):
+                normalise(n, 0)
+                normalise(n, 1)
+            if n == 0:
+                for i in (0, 1, 2, 3):
+                    wb_prepare(i, "SSSS"[i])
+            if is_pair(n - 1):
+                copy_out(last[0], 0, "S")
+                copy_out(last[0], 1, "V")
+                copy_out(last[1], 0, "S")
+                copy_out(last[1], 1, "S")
+                store(n - 1, 0, 2)

@@ -33,12 +33,15 @@ def tile_multiheadlatentattention_pb_t_kernel(tc, x, w_kva, kva_norm_w, w_kvb, o
         engines = {"S": nc.scalar.copy, "V": nc.vector.tensor_copy}
         live = {}
 
-        state = {"g": 0}
+        state = {"g": 0, "l": 0}
 
         def bank(shape, name, tag="G"):
             if tag == "G":
                 tag = "G%d" % (state["g"] % 5)
                 state["g"] = state["g"] + 1
+            if tag == "L":
+                tag = "L%d" % (state["l"] % 3)
+                state["l"] = state["l"] + 1
             return psum.tile(shape, F32, name=name, tag=tag)
 
         pos_i = const.tile([P, TPP], I32, name="pos_i")
@@ -73,8 +76,8 @@ def tile_multiheadlatentattention_pb_t_kernel(tc, x, w_kva, kva_norm_w, w_kvb, o
             )
             wa_words.append(wa_raw[:].bitcast(F32))
             if u == 0:
+                nc.sync.dma_start(out=g_row[0:1, :], in_=kva_norm_w.rearrange("(o k) -> o k", o=1))
                 load_x(0, 1)
-        nc.scalar.dma_start(out=g_row[0:1, :], in_=kva_norm_w.rearrange("(o k) -> o k", o=1))
         wr_raw = const.tile([P, C], BF16, name="wr_raw")
         nc.sync.dma_start(out=wr_raw[:], in_=w_kva[KVL : KVL + R, :])
         load_x(1, 1)
@@ -89,14 +92,19 @@ def tile_multiheadlatentattention_pb_t_kernel(tc, x, w_kva, kva_norm_w, w_kvb, o
 
         tab = const.tile([P, TPP, 3, 64], F32, name="tab")
         turns = const.tile([P, TPP, 64], F32, name="turns")
-        nc.vector.tensor_scalar(
-            out=turns[:, :, 0], in0=pos_i[:], scalar1=1.0 / (2.0 * math.pi), scalar2=None, op0=ALU.mult
-        )
-        for s in range(6):
-            n = 2**s
+        for s in range(4):
             nc.vector.tensor_scalar(
-                out=turns[:, :, n : 2 * n], in0=turns[:, :, 0:n], scalar1=RATIO**n, scalar2=None, op0=ALU.mult
+                out=turns[:, :, s], in0=pos_i[:], scalar1=RATIO**s / (2.0 * math.pi), scalar2=None, op0=ALU.mult
             )
+        for n in (4, 16):
+            for s in range(1, 4):
+                nc.vector.tensor_scalar(
+                    out=turns[:, :, n * s : n * s + n],
+                    in0=turns[:, :, 0:n],
+                    scalar1=RATIO ** (n * s),
+                    scalar2=None,
+                    op0=ALU.mult,
+                )
         whole = const.tile([P, TPP, 64], I32, name="whole")
         nc.vector.tensor_copy(out=whole[:], in_=turns[:])
         frac = const.tile([P, TPP, 64], F32, name="frac")
@@ -156,9 +164,11 @@ def tile_multiheadlatentattention_pb_t_kernel(tc, x, w_kva, kva_norm_w, w_kvb, o
             cols = slice(KVL * g + 256 * u, KVL * g + 256 * u + 256)
             quantise(wl_q[:, cols], wl_s[:, cols], grp[:])
 
-        def wr_prepare(eng):
+        def wr_transpose():
             words = wr_raw[:].bitcast(F32)
-            ps = transposes(every_2nd(words, 0) + every_2nd(words, 256), "wr_ps")
+            return transposes(every_2nd(words, 0) + every_2nd(words, 256), "wr_ps")
+
+        def wr_finish(ps, eng):
             grp = stage.tile([P, 1024], BF16, name="wgrp", tag="wgrp", align_bytes=64)
             interleave(ps, grp[:], eng)
             quantise(wr_q[:], wr_s[:], grp[:])
@@ -173,24 +183,22 @@ def tile_multiheadlatentattention_pb_t_kernel(tc, x, w_kva, kva_norm_w, w_kvb, o
             quantise(wb_q[:, cols], wb_s[:, cols], grp[:])
 
         def gain():
-            g_ps = bank([P, KVL], "g_ps", "RC")
+            g_ps = bank([P, KVL], "g_ps")
             nc.tensor.matmul(out=g_ps[:], lhsT=ones[:], rhs=g_row[:], start=True, stop=True)
             nc.scalar.copy(
                 out=g_bc[:].rearrange("p (u m e) -> p u m e", u=2, e=2),
                 in_=g_ps[:].rearrange("p (m u e) -> p u m e", u=2, e=2),
             )
 
-        def x_transpose(q):
-            live["xt", q] = [
-                transposes(every_2nd(x_words[2 * q + a], 0) + every_2nd(x_words[2 * q + a], 256), "xt")
-                for a in range(2)
-            ]
+        def x_transpose(q, a):
+            words = x_words[2 * q + a]
+            live["xt", q, a] = transposes(every_2nd(words, 0) + every_2nd(words, 256), "xt")
 
         def x_copy(q, a, eng):
             if a == 0:
                 xg = stage.tile([P, 2048], BF16, name="xg", tag="xgrp", align_bytes=64)
                 live["xg", q] = xg
-            interleave(live["xt", q][a], live["xg", q][:, 1024 * a : 1024 * a + 1024], eng)
+            interleave(live["xt", q, a], live["xg", q][:, 1024 * a : 1024 * a + 1024], eng)
 
         def x_quantise(q):
             xq = ring.tile([P, 512], U32, name="xq", tag="xq", align_bytes=64)
@@ -212,14 +220,14 @@ def tile_multiheadlatentattention_pb_t_kernel(tc, x, w_kva, kva_norm_w, w_kvb, o
             )
 
         def stage1_latent(q, a):
-            l = bank([P, KVL], "l", "L%d" % a)
+            l = bank([P, KVL], "l", "L")
             for g in range(2):
                 cols = slice(KVL * g, KVL * g + KVL)
                 stage1_pass(l[:], q, a, g, wl_q[:, cols], wl_s[:, cols])
             live["l", q, a] = l
 
         def stage1_rotary(q):
-            r_ps = bank([P, 2, R], "r_ps", "RC")
+            r_ps = bank([P, 2, R], "r_ps")
             for a in range(2):
                 for g in range(2):
                     cols = slice(R * g, R * g + R)
@@ -260,7 +268,7 @@ def tile_multiheadlatentattention_pb_t_kernel(tc, x, w_kva, kva_norm_w, w_kvb, o
             for t in tiles:
                 words = live["c", t][:].bitcast(F32)
                 blocks = blocks + [words[:, P * v : P * v + P] for v in range(2)]
-            live["ct", tiles] = transposes(blocks, "ct", "RC")
+            live["ct", tiles] = transposes(blocks, "ct")
 
         def c_copy(tiles, eng):
             w = len(tiles)
@@ -294,9 +302,6 @@ def tile_multiheadlatentattention_pb_t_kernel(tc, x, w_kva, kva_norm_w, w_kvb, o
 
         def rotate(q):
             t0 = 2 * (q % 4)
-            k_sb = outp.tile([P, 2, H, 256], F32, name="k_sb", tag="k_sb")
-            v_sb = outp.tile([P, 2, H * 128], F32, name="v_sb", tag="v_sb")
-            live["out", q] = (k_sb, v_sb)
             r_pairs = live["r", q][:].rearrange("p t (j e) -> p t e j", e=2)
             products = []
             for e in range(2):
@@ -309,6 +314,11 @@ def tile_multiheadlatentattention_pb_t_kernel(tc, x, w_kva, kva_norm_w, w_kvb, o
                 )
                 products.append(m)
             live["m", q] = products
+
+        def open_out(q):
+            k_sb = outp.tile([P, 2, H, 256], F32, name="k_sb", tag="k_sb")
+            v_sb = outp.tile([P, 2, H * 128], F32, name="v_sb", tag="v_sb")
+            live["out", q] = (k_sb, v_sb)
 
         def rotate_add(q, eng):
             k_sb = live["out", q][0]
@@ -354,7 +364,8 @@ def tile_multiheadlatentattention_pb_t_kernel(tc, x, w_kva, kva_norm_w, w_kvb, o
             return 0 <= q < N_PAIRS
 
         wa0 = [wa_transpose(0, g) for g in range(2)]
-        x_transpose(0)
+        x_transpose(0, 0)
+        x_transpose(0, 1)
         grp0 = [wa_copy(wa0[g], "V") for g in range(2)]
         for g in range(2):
             wa_quantise(0, g, grp0[g])
@@ -367,48 +378,65 @@ def tile_multiheadlatentattention_pb_t_kernel(tc, x, w_kva, kva_norm_w, w_kvb, o
             wa_quantise(1, g, grp1[g])
         warm = const.tile([P, 1], F32, name="warm")
         nc.scalar.activation(out=warm[:], in_=eps_t[:], func=ACT.Abs_reciprocal_sqrt)
-        wr_prepare("V")
+        wr = wr_transpose()
 
-        for n in range(N_PAIRS + 1):
-            last = (2 * n - 2, 2 * n - 1)
-            if is_pair(n + 1):
-                x_transpose(n + 1)
-            if is_pair(n - 1):
-                c_transpose(last)
-            if is_pair(n + 1):
-                x_copy(n + 1, 0, "S")
+        for n in range(-1, N_PAIRS + 3):
+            prev = (2 * n - 4, 2 * n - 3)
+            old = (2 * n - 6, 2 * n - 5)
+            if is_pair(n - 2):
+                c_transpose(prev)
+            if is_pair(n + 1) and n >= 0:
+                x_transpose(n + 1, 1)
+            if is_pair(n - 2):
+                c_copy(prev, "S")
+            if is_pair(n + 1) and n >= 0:
                 x_copy(n + 1, 1, "S")
+            if is_pair(n - 3):
+                stage2(old, 1, 1)
+                stage2(old, 1, 0)
+                stage2(old, 0, 0)
+                copy_out(old[1], 1, "S")
+                copy_out(old[0], 0, "S")
+                copy_out(old[1], 0, "V")
+                store(n - 3, 0, 2)
+            if is_pair(n - 2):
+                c_quantise(prev)
             if is_pair(n - 1):
-                c_copy(last, "V")
-                c_quantise(last)
-            if is_pair(n + 1):
+                normalise(n - 1, 1)
+            if is_pair(n + 1) and n >= 0:
                 x_quantise(n + 1)
             if is_pair(n):
                 stage1_latent(n, 0)
-                stage1_latent(n, 1)
-                stage1_rotary(n)
-                squares(n)
-                inverse_rms(n)
-            if n == 0:
-                gain()
-                finish_tables()
-            if is_pair(n):
-                rotate(n)
-                rotate_add(n, nc.gpsimd)
-                rotate_spread(n, [(1, 4)])
             if is_pair(n - 1):
-                for i in range(2):
-                    for part in range(2):
-                        stage2(last, i, part)
+                stage1_rotary(n - 1)
+            if is_pair(n):
+                stage1_latent(n, 1)
+            if n == -1:
+                gain()
+            if n == 0:
+                wr_finish(wr, "S")
+                finish_tables()
+            if is_pair(n - 1):
+                rotate(n - 1)
+            if is_pair(n):
+                squares(n)
+            if is_pair(n - 2):
+                stage2(prev, 0, 1)
+                open_out(n - 2)
+                copy_out(prev[0], 1, "S")
+            if is_pair(n):
+                inverse_rms(n)
+            if is_pair(n - 2):
+                rotate_add(n - 2, nc.vector)
+                rotate_spread(n - 2, [(1, 4)])
+            if is_pair(n + 2):
+                x_transpose(n + 2, 0)
+                x_copy(n + 2, 0, "V")
             if is_pair(n):
                 normalise(n, 0)
-                normalise(n, 1)
             if n == 0:
-                for i in (0, 1, 2, 3):
-                    wb_prepare(i, "SSSS"[i])
-            if is_pair(n - 1):
-                copy_out(last[0], 0, "S")
-                copy_out(last[0], 1, "V")
-                copy_out(last[1], 0, "S")
-                copy_out(last[1], 1, "S")
-                store(n - 1, 0, 2)
+                for i in range(2, 4):
+                    wb_prepare(i, "S")
+            if n == 1:
+                for i in range(2):
+                    wb_prepare(i, "S")

@@ -26,7 +26,7 @@ FLOPS = 2 * B * T * C * (KVL + R) + 2 * B * T * KVL * (H * 256)
 def tile_multiheadlatentattention_pb_t_kernel(tc, x, w_kva, kva_norm_w, w_kvb, out_0, out_1):
     nc = tc.nc
     with tc.tile_pool(name="const", bufs=1) as const, tc.tile_pool(name="stage", bufs=3) as stage, tc.tile_pool(
-        name="ring", bufs=7
+        name="ring", bufs=6
     ) as ring, tc.tile_pool(name="work", bufs=3) as work, tc.tile_pool(name="small", bufs=4) as small, tc.tile_pool(
         name="outp", bufs=5
     ) as outp, tc.psum_pool(name="psum", bufs=1) as psum, tc.manual_schedule():
@@ -173,18 +173,24 @@ def tile_multiheadlatentattention_pb_t_kernel(tc, x, w_kva, kva_norm_w, w_kvb, o
             interleave(ps, grp[:], eng)
             quantise(wr_q[:], wr_s[:], grp[:])
 
-        def wb_prepare(i, eng):
+        def wb_start(i, eng):
             words = wb_raw[:].bitcast(F32)
             ra, rb = ((0, 2), (4, 6), (1, 3), (5, 7))[i]
             ps = transposes(every_2nd(words, 256 * ra) + every_2nd(words, 256 * rb), "wb_ps")
             grp = stage.tile([P, 1024], BF16, name="wgrp", tag="wgrp", align_bytes=64)
             interleave(ps, grp[:], eng)
-            cols = slice(256 * i, 256 * i + 256)
-            quantise(wb_q[:, cols], wb_s[:, cols], grp[:])
+            live["wb", i] = grp
 
-        def gain():
+        def wb_quantise(i):
+            cols = slice(256 * i, 256 * i + 256)
+            quantise(wb_q[:, cols], wb_s[:, cols], live["wb", i][:])
+
+        def gain_spread():
             g_ps = bank([P, KVL], "g_ps")
             nc.tensor.matmul(out=g_ps[:], lhsT=ones[:], rhs=g_row[:], start=True, stop=True)
+            return g_ps
+
+        def gain_copy(g_ps):
             nc.scalar.copy(
                 out=g_bc[:].rearrange("p (u m e) -> p u m e", u=2, e=2),
                 in_=g_ps[:].rearrange("p (m u e) -> p u m e", u=2, e=2),
@@ -195,7 +201,7 @@ def tile_multiheadlatentattention_pb_t_kernel(tc, x, w_kva, kva_norm_w, w_kvb, o
             live["xt", q, a] = transposes(every_2nd(words, 0) + every_2nd(words, 256), "xt")
 
         def x_copy(q, a, eng):
-            if a == 0:
+            if ("xg", q) not in live:
                 xg = stage.tile([P, 2048], BF16, name="xg", tag="xgrp", align_bytes=64)
                 live["xg", q] = xg
             interleave(live["xt", q, a], live["xg", q][:, 1024 * a : 1024 * a + 1024], eng)
@@ -237,7 +243,7 @@ def tile_multiheadlatentattention_pb_t_kernel(tc, x, w_kva, kva_norm_w, w_kvb, o
         def squares(q):
             ssq = small.tile([P, 2], F32, name="ssq", tag="ssq")
             live["ssq", q] = ssq
-            for a in range(2):
+            for a in (1, 0):
                 junk = work.tile([P, KVL], BF16, name="junk", tag="junk")
                 nc.scalar.activation(
                     out=junk[:], in_=live["l", q, a][:], func=ACT.Square, accum_out=ssq[:, a : a + 1]
@@ -351,14 +357,14 @@ def tile_multiheadlatentattention_pb_t_kernel(tc, x, w_kva, kva_norm_w, w_kvb, o
             else:
                 engines[eng](out=v_sb[:, a, :], in_=kv[:])
 
-        def store(q, lo, hi):
-            k_sb, v_sb = live["out", q]
-            b = q // 4
+        def store_k(q):
             t0 = 2 * (q % 4)
-            nc.sync.dma_start(
-                out=k_rows[b][:, t0 + lo : t0 + hi, :], in_=k_sb[:, lo:hi].rearrange("p t h d -> p t (h d)")
-            )
-            nc.sync.dma_start(out=v_rows[b][:, t0 + lo : t0 + hi, :], in_=v_sb[:, lo:hi, :])
+            k_sb = live["out", q][0]
+            nc.sync.dma_start(out=k_rows[q // 4][:, t0 : t0 + 2, :], in_=k_sb[:].rearrange("p t h d -> p t (h d)"))
+
+        def store_v(q):
+            t0 = 2 * (q % 4)
+            nc.sync.dma_start(out=v_rows[q // 4][:, t0 : t0 + 2, :], in_=live["out", q][1][:])
 
         def is_pair(q):
             return 0 <= q < N_PAIRS
@@ -376,67 +382,69 @@ def tile_multiheadlatentattention_pb_t_kernel(tc, x, w_kva, kva_norm_w, w_kvb, o
         grp1 = [wa_copy(wa1[g], "SV"[g]) for g in range(2)]
         for g in range(2):
             wa_quantise(1, g, grp1[g])
+        gain_ps = gain_spread()
         warm = const.tile([P, 1], F32, name="warm")
         nc.scalar.activation(out=warm[:], in_=eps_t[:], func=ACT.Abs_reciprocal_sqrt)
         wr = wr_transpose()
 
-        for n in range(-1, N_PAIRS + 3):
+        gain_copy(gain_ps)
+        wr_finish(wr, "V")
+        finish_tables()
+        for n in range(N_PAIRS + 3):
             prev = (2 * n - 4, 2 * n - 3)
             old = (2 * n - 6, 2 * n - 5)
             if is_pair(n - 2):
                 c_transpose(prev)
-            if is_pair(n + 1) and n >= 0:
+            if is_pair(n + 1):
                 x_transpose(n + 1, 1)
+                x_transpose(n + 1, 0)
             if is_pair(n - 2):
                 c_copy(prev, "S")
-            if is_pair(n + 1) and n >= 0:
+            if is_pair(n + 1):
                 x_copy(n + 1, 1, "S")
-            if is_pair(n - 3):
-                stage2(old, 1, 1)
-                stage2(old, 1, 0)
-                stage2(old, 0, 0)
-                copy_out(old[1], 1, "S")
-                copy_out(old[0], 0, "S")
-                copy_out(old[1], 0, "V")
-                store(n - 3, 0, 2)
+                x_copy(n + 1, 0, "S")
+            if n == 1:
+                for i in (2, 3):
+                    wb_start(i, "S")
             if is_pair(n - 2):
                 c_quantise(prev)
-            if is_pair(n - 1):
-                normalise(n - 1, 1)
-            if is_pair(n + 1) and n >= 0:
+            if is_pair(n - 3):
+                stage2(old, 0, 0)
+                copy_out(old[0], 0, "S")
+                store_k(n - 3)
+            if is_pair(n - 2):
+                stage1_rotary(n - 2)
+                rotate(n - 2)
+                open_out(n - 2)
+                rotate_add(n - 2, nc.gpsimd)
+                rotate_spread(n - 2, [(1, 4)])
+            if is_pair(n + 1):
                 x_quantise(n + 1)
-            if is_pair(n):
-                stage1_latent(n, 0)
-            if is_pair(n - 1):
-                stage1_rotary(n - 1)
+            if n == 1:
+                for i in (2, 3):
+                    wb_quantise(i)
             if is_pair(n):
                 stage1_latent(n, 1)
-            if n == -1:
-                gain()
-            if n == 0:
-                wr_finish(wr, "S")
-                finish_tables()
-            if is_pair(n - 1):
-                rotate(n - 1)
-            if is_pair(n):
+                stage1_latent(n, 0)
                 squares(n)
+            if n == 0:
+                wb_start(0, "S")
+                wb_start(1, "V")
+            if is_pair(n - 3):
+                stage2(old, 0, 1)
             if is_pair(n - 2):
-                stage2(prev, 0, 1)
-                open_out(n - 2)
-                copy_out(prev[0], 1, "S")
+                stage2(prev, 1, 0)
+                copy_out(prev[1], 0, "S")
             if is_pair(n):
                 inverse_rms(n)
-            if is_pair(n - 2):
-                rotate_add(n - 2, nc.vector)
-                rotate_spread(n - 2, [(1, 4)])
-            if is_pair(n + 2):
-                x_transpose(n + 2, 0)
-                x_copy(n + 2, 0, "V")
+            if is_pair(n - 3):
+                stage2(old, 1, 1)
+                copy_out(old[0], 1, "V")
+                copy_out(old[1], 1, "V")
+                store_v(n - 3)
             if is_pair(n):
+                normalise(n, 1)
                 normalise(n, 0)
             if n == 0:
-                for i in range(2, 4):
-                    wb_prepare(i, "S")
-            if n == 1:
-                for i in range(2):
-                    wb_prepare(i, "S")
+                wb_quantise(0)
+                wb_quantise(1)

@@ -121,12 +121,12 @@ def tile_multiheadlatentattention_pb_t_kernel(tc, x, w_kva, kva_norm_w, w_kvb, o
             )
             nc.vector.tensor_scalar(out=tab[:, :, 1, :], in0=sq_h[:], scalar1=1.0, scalar2=None, op0=ALU.add)
 
-        wl_q = const.tile([P, 2 * KVL], U32, name="wl_q", align_bytes=64)
-        wl_s = const.tile([P, 2 * KVL], U8, name="wl_s", align_bytes=64)
-        wr_q = const.tile([P, 2 * R], U32, name="wr_q", align_bytes=64)
-        wr_s = const.tile([P, 2 * R], U8, name="wr_s", align_bytes=64)
-        wb_q = const.tile([P, 1024], U32, name="wb_q", align_bytes=64)
-        wb_s = const.tile([P, 1024], U8, name="wb_s", align_bytes=64)
+        wl_q = const.tile([P, 2 * KVL], U32, name="wl_q", align_bytes=256)
+        wl_s = const.tile([P, 2 * KVL], U8, name="wl_s", align_bytes=256)
+        wr_q = const.tile([P, 2 * R], U32, name="wr_q", align_bytes=256)
+        wr_s = const.tile([P, 2 * R], U8, name="wr_s", align_bytes=256)
+        wb_q = const.tile([P, 1024], U32, name="wb_q", align_bytes=256)
+        wb_s = const.tile([P, 1024], U8, name="wb_s", align_bytes=256)
         g_bc = const.tile([P, KVL], BF16, name="g_bc")
 
         def transposes(blocks, name, tag="G"):
@@ -207,8 +207,8 @@ def tile_multiheadlatentattention_pb_t_kernel(tc, x, w_kva, kva_norm_w, w_kvb, o
             interleave(live["xt", q, a], live["xg", q][:, 1024 * a : 1024 * a + 1024], eng)
 
         def x_quantise(q):
-            xq = ring.tile([P, 512], U32, name="xq", tag="xq", align_bytes=64)
-            xs = ring.tile([P, 512], U8, name="xs", tag="xs", align_bytes=64)
+            xq = ring.tile([P, 512], U32, name="xq", tag="xq", align_bytes=256)
+            xs = ring.tile([P, 512], U8, name="xs", tag="xs", align_bytes=256)
             quantise(xq[:], xs[:], live["xg", q][:])
             live["xq", q] = (xq, xs)
 
@@ -287,8 +287,8 @@ def tile_multiheadlatentattention_pb_t_kernel(tc, x, w_kva, kva_norm_w, w_kvb, o
 
         def c_quantise(tiles):
             w = len(tiles)
-            cq = work.tile([P, 256], U32, name="cq", tag="cq", align_bytes=64)
-            cs = work.tile([P, 256], U8, name="cs", tag="cs", align_bytes=64)
+            cq = work.tile([P, 256], U32, name="cq", tag="cq", align_bytes=256)
+            cs = work.tile([P, 256], U8, name="cs", tag="cs", align_bytes=256)
             quantise(cq[:, 0 : P * w], cs[:, 0 : P * w], live["cg", tiles][:, 0 : 512 * w])
             live["cq", tiles] = (cq, cs)
 

@@ -168,10 +168,10 @@ def tile_multiheadlatentattention_pb_t_kernel(tc, x, w_kva, kva_norm_w, w_kvb, o
             words = wr_raw[:].bitcast(F32)
             return transposes(every_2nd(words, 0) + every_2nd(words, 256), "wr_ps")
 
-        def wr_finish(ps, eng):
+        def wr_copy(ps, eng):
             grp = stage.tile([P, 1024], BF16, name="wgrp", tag="wgrp", align_bytes=64)
             interleave(ps, grp[:], eng)
-            quantise(wr_q[:], wr_s[:], grp[:])
+            return grp
 
         def wb_start(i, eng):
             words = wb_raw[:].bitcast(F32)
@@ -191,7 +191,7 @@ def tile_multiheadlatentattention_pb_t_kernel(tc, x, w_kva, kva_norm_w, w_kvb, o
             return g_ps
 
         def gain_copy(g_ps):
-            nc.scalar.copy(
+            nc.vector.tensor_copy(
                 out=g_bc[:].rearrange("p (u m e) -> p u m e", u=2, e=2),
                 in_=g_ps[:].rearrange("p (m u e) -> p u m e", u=2, e=2),
             )
@@ -240,29 +240,29 @@ def tile_multiheadlatentattention_pb_t_kernel(tc, x, w_kva, kva_norm_w, w_kvb, o
                     stage1_pass(r_ps[:, a, :], q, a, g, wr_q[:, cols], wr_s[:, cols])
             live["r", q] = r_ps
 
-        def squares(q):
-            ssq = small.tile([P, 2], F32, name="ssq", tag="ssq")
-            live["ssq", q] = ssq
-            for a in (1, 0):
-                junk = work.tile([P, KVL], BF16, name="junk", tag="junk")
-                nc.scalar.activation(
-                    out=junk[:], in_=live["l", q, a][:], func=ACT.Square, accum_out=ssq[:, a : a + 1]
-                )
+        def squares(q, a):
+            ssq = small.tile([P, 1], F32, name="ssq", tag="ssq%d" % a)
+            junk = work.tile([P, KVL], BF16, name="junk", tag="junk")
+            nc.scalar.activation(out=junk[:], in_=live["l", q, a][:], func=ACT.Square, accum_out=ssq[:])
+            live["ssq", q, a] = ssq
 
-        def inverse_rms(q):
-            ssq = live["ssq", q]
-            rstd = small.tile([P, 2], F32, name="rstd", tag="rstd")
+        def inverse_rms(q, a):
+            rstd = small.tile([P, 1], F32, name="rstd", tag="rstd%d" % a)
             nc.scalar.activation(
-                out=rstd[:], in_=ssq[:], func=ACT.Abs_reciprocal_sqrt, scale=1.0 / KVL, bias=eps_t[:, 0:1]
+                out=rstd[:],
+                in_=live["ssq", q, a][:],
+                func=ACT.Abs_reciprocal_sqrt,
+                scale=1.0 / KVL,
+                bias=eps_t[:, 0:1],
             )
-            live["rstd", q] = rstd
+            live["rstd", q, a] = rstd
 
         def normalise(q, a):
             c_sb = work.tile([P, KVL], BF16, name="c_sb", tag="c_sb", bufs=6)
             nc.vector.scalar_tensor_tensor(
                 out=c_sb[:],
                 in0=live["l", q, a][:],
-                scalar=live["rstd", q][:, a : a + 1],
+                scalar=live["rstd", q, a][:],
                 in1=g_bc[:],
                 op0=ALU.mult,
                 op1=ALU.mult,
@@ -357,14 +357,16 @@ def tile_multiheadlatentattention_pb_t_kernel(tc, x, w_kva, kva_norm_w, w_kvb, o
             else:
                 engines[eng](out=v_sb[:, a, :], in_=kv[:])
 
-        def store_k(q):
+        def store_k(q, a0=0, a1=2):
             t0 = 2 * (q % 4)
-            k_sb = live["out", q][0]
-            nc.sync.dma_start(out=k_rows[q // 4][:, t0 : t0 + 2, :], in_=k_sb[:].rearrange("p t h d -> p t (h d)"))
+            nc.sync.dma_start(
+                out=k_rows[q // 4][:, t0 + a0 : t0 + a1, :],
+                in_=live["out", q][0][:, a0:a1].rearrange("p t h d -> p t (h d)"),
+            )
 
-        def store_v(q):
+        def store_v(q, a0=0, a1=2):
             t0 = 2 * (q % 4)
-            nc.sync.dma_start(out=v_rows[q // 4][:, t0 : t0 + 2, :], in_=live["out", q][1][:])
+            nc.sync.dma_start(out=v_rows[q // 4][:, t0 + a0 : t0 + a1, :], in_=live["out", q][1][:, a0:a1, :])
 
         def is_pair(q):
             return 0 <= q < N_PAIRS
@@ -378,73 +380,65 @@ def tile_multiheadlatentattention_pb_t_kernel(tc, x, w_kva, kva_norm_w, w_kvb, o
         x_copy(0, 0, "S")
         x_copy(0, 1, "S")
         wa1 = [wa_transpose(1, g) for g in range(2)]
-        x_quantise(0)
         grp1 = [wa_copy(wa1[g], "SV"[g]) for g in range(2)]
+        x_quantise(0)
         for g in range(2):
             wa_quantise(1, g, grp1[g])
         gain_ps = gain_spread()
         warm = const.tile([P, 1], F32, name="warm")
         nc.scalar.activation(out=warm[:], in_=eps_t[:], func=ACT.Abs_reciprocal_sqrt)
-        wr = wr_transpose()
-
         gain_copy(gain_ps)
-        wr_finish(wr, "V")
+        wr_grp = wr_copy(wr_transpose(), "V")
         finish_tables()
+
         for n in range(N_PAIRS + 3):
             prev = (2 * n - 4, 2 * n - 3)
             old = (2 * n - 6, 2 * n - 5)
+            if is_pair(n + 1):
+                for a in range(2):
+                    x_transpose(n + 1, a)
+                    x_copy(n + 1, a, "S")
             if is_pair(n - 2):
                 c_transpose(prev)
-            if is_pair(n + 1):
-                x_transpose(n + 1, 1)
-                x_transpose(n + 1, 0)
-            if is_pair(n - 2):
                 c_copy(prev, "S")
-            if is_pair(n + 1):
-                x_copy(n + 1, 1, "S")
-                x_copy(n + 1, 0, "S")
-            if n == 1:
-                for i in (2, 3):
-                    wb_start(i, "S")
-            if is_pair(n - 2):
-                c_quantise(prev)
             if is_pair(n - 3):
-                stage2(old, 0, 0)
-                copy_out(old[0], 0, "S")
-                store_k(n - 3)
+                stage2(old, 0, 1)
+                copy_out(old[0], 1, "V")
             if is_pair(n - 2):
                 stage1_rotary(n - 2)
                 rotate(n - 2)
                 open_out(n - 2)
                 rotate_add(n - 2, nc.gpsimd)
                 rotate_spread(n - 2, [(1, 4)])
+                c_quantise(prev)
+            if is_pair(n - 3):
+                stage2(old, 0, 0)
+                copy_out(old[0], 0, "S")
             if is_pair(n + 1):
                 x_quantise(n + 1)
-            if n == 1:
-                for i in (2, 3):
-                    wb_quantise(i)
             if is_pair(n):
                 stage1_latent(n, 1)
                 stage1_latent(n, 0)
-                squares(n)
-            if n == 0:
-                wb_start(0, "S")
-                wb_start(1, "V")
-            if is_pair(n - 3):
-                stage2(old, 0, 1)
-            if is_pair(n - 2):
-                stage2(prev, 1, 0)
-                copy_out(prev[1], 0, "S")
-            if is_pair(n):
-                inverse_rms(n)
+                squares(n, 1)
+                squares(n, 0)
+                inverse_rms(n, 1)
             if is_pair(n - 3):
                 stage2(old, 1, 1)
-                copy_out(old[0], 1, "V")
                 copy_out(old[1], 1, "V")
                 store_v(n - 3)
-            if is_pair(n):
-                normalise(n, 1)
-                normalise(n, 0)
+                stage2(old, 1, 0)
+                copy_out(old[1], 0, "S")
+                store_k(n - 3)
             if n == 0:
-                wb_quantise(0)
-                wb_quantise(1)
+                quantise(wr_q[:], wr_s[:], wr_grp[:])
+            if n < 2:
+                wb_start(2 * n, "S")
+            if is_pair(n):
+                inverse_rms(n, 0)
+                normalise(n, 1)
+            if n < 2:
+                wb_start(2 * n + 1, "V")
+                wb_quantise(2 * n)
+                wb_quantise(2 * n + 1)
+            if is_pair(n):
+                normalise(n, 0)

@@ -61,34 +61,33 @@ def tile_multiheadlatentattention_pb_t_kernel(tc, x, w_kva, kva_norm_w, w_kvb, o
         wa_rows = w_kva[0:KVL, :].rearrange("(m s) k -> m s k", s=4)
         x_words = {}
 
-        def load_x(q, pairs):
-            xr = const.tile([P, 2 * pairs * C], BF16, name="x_%d" % q)
-            nc.sync.dma_start(out=xr[:], in_=x_rows[q // 4][:, 2 * C * (q % 4) : 2 * C * (q % 4 + pairs)])
+        def load_x(t, tiles):
+            xr = const.tile([P, tiles * C], BF16, name="x_%d" % t)
+            nc.sync.dma_start(out=xr[:], in_=x_rows[t // TPP][:, C * (t % TPP) : C * (t % TPP + tiles)])
             words = xr[:].bitcast(F32)
-            for i in range(2 * pairs):
-                x_words[2 * q + i] = words[:, 512 * i : 512 * i + 512]
+            for i in range(tiles):
+                x_words[t + i] = words[:, 512 * i : 512 * i + 512]
 
         wa_words = []
-        for u in range(2):
-            wa_raw = const.tile([P, 2 * C], BF16, name="wa_raw%d" % u)
-            nc.sync.dma_start(
-                out=wa_raw[:].rearrange("p (s k) -> p s k", s=2), in_=wa_rows[:, 2 * u : 2 * u + 2, :]
-            )
+        for s in range(4):
+            wa_raw = const.tile([P, C], BF16, name="wa_raw%d" % s)
+            nc.sync.dma_start(out=wa_raw[:], in_=wa_rows[:, s, :])
             wa_words.append(wa_raw[:].bitcast(F32))
-            if u == 0:
+            if s == 1:
                 nc.sync.dma_start(out=g_row[0:1, :], in_=kva_norm_w.rearrange("(o k) -> o k", o=1))
-                load_x(0, 1)
+        load_x(0, 1)
+        load_x(1, 1)
         wr_raw = const.tile([P, C], BF16, name="wr_raw")
         nc.sync.dma_start(out=wr_raw[:], in_=w_kva[KVL : KVL + R, :])
-        load_x(1, 1)
+        load_x(2, 2)
         wb_raw = const.tile([P, 8 * KVL], BF16, name="wb_raw")
         nc.sync.dma_start(
             out=wb_raw[:].rearrange("p (r k) -> p r k", r=8), in_=w_kvb.rearrange("(r p) k -> p r k", p=P)
         )
-        load_x(2, 1)
-        load_x(3, 1)
-        for q in range(4, N_PAIRS, 2):
-            load_x(q, 2)
+        load_x(4, 2)
+        load_x(6, 2)
+        for t in range(8, 2 * N_PAIRS, 4):
+            load_x(t, 4)
 
         tab = const.tile([P, TPP, 3, 64], F32, name="tab")
         turns = const.tile([P, TPP, 64], F32, name="turns")
@@ -112,12 +111,14 @@ def tile_multiheadlatentattention_pb_t_kernel(tc, x, w_kva, kva_norm_w, w_kvb, o
         sin_h = const.tile([P, TPP, 64], F32, name="sin_h")
         nc.scalar.activation(out=sin_h[:], in_=frac[:], func=ACT.Sin, scale=math.pi)
         nc.scalar.activation(out=tab[:, :, 2, :], in_=frac[:], func=ACT.Sin, scale=2.0 * math.pi)
-        nc.scalar.activation(out=tab[:, :, 0, :], in_=frac[:], func=ACT.Sin, scale=-2.0 * math.pi)
         sq_h = const.tile([P, TPP, 64], F32, name="sq_h")
 
         def finish_tables():
             nc.vector.scalar_tensor_tensor(
                 out=sq_h[:], in0=sin_h[:], scalar=-2.0, in1=sin_h[:], op0=ALU.mult, op1=ALU.mult
+            )
+            nc.vector.tensor_scalar(
+                out=tab[:, :, 0, :], in0=tab[:, :, 2, :], scalar1=-1.0, scalar2=None, op0=ALU.mult
             )
             nc.vector.tensor_scalar(out=tab[:, :, 1, :], in0=sq_h[:], scalar1=1.0, scalar2=None, op0=ALU.add)
 
@@ -147,10 +148,15 @@ def tile_multiheadlatentattention_pb_t_kernel(tc, x, w_kva, kva_norm_w, w_kvb, o
         def quantise(codes, scales, src):
             nc.vector.quantize_mx(out=codes.bitcast(FP8X4), scales=scales, in_=src)
 
-        def wa_transpose(u, g):
-            return transposes(
-                every_2nd(wa_words[u], 256 * g) + every_2nd(wa_words[u], 512 + 256 * g), "wa_ps"
-            )
+        def wa_transpose(u):
+            banks = [bank([P, 512], "wa_ps") for g in range(2)]
+            for e in range(2):
+                for g in range(2):
+                    for v, words in enumerate(every_2nd(wa_words[2 * u + e], 256 * g)):
+                        nc.tensor.transpose(
+                            out=banks[g][:, P * (2 * e + v) : P * (2 * e + v) + P], in_=words, identity=ident[:]
+                        )
+            return banks
 
         def wa_copy(ps, eng):
             grp = stage.tile([P, 1024], BF16, name="wgrp", tag="wgrp", align_bytes=64)
@@ -371,19 +377,19 @@ def tile_multiheadlatentattention_pb_t_kernel(tc, x, w_kva, kva_norm_w, w_kvb, o
         def is_pair(q):
             return 0 <= q < N_PAIRS
 
-        wa0 = [wa_transpose(0, g) for g in range(2)]
+        wa0 = wa_transpose(0)
+        wa1 = wa_transpose(1)
         x_transpose(0, 0)
-        x_transpose(0, 1)
         grp0 = [wa_copy(wa0[g], "V") for g in range(2)]
         for g in range(2):
             wa_quantise(0, g, grp0[g])
-        x_copy(0, 0, "S")
-        x_copy(0, 1, "S")
-        wa1 = [wa_transpose(1, g) for g in range(2)]
         grp1 = [wa_copy(wa1[g], "SV"[g]) for g in range(2)]
-        x_quantise(0)
+        x_copy(0, 0, "S")
+        x_transpose(0, 1)
+        x_copy(0, 1, "S")
         for g in range(2):
             wa_quantise(1, g, grp1[g])
+        x_quantise(0)
         gain_ps = gain_spread()
         warm = const.tile([P, 1], F32, name="warm")
         nc.scalar.activation(out=warm[:], in_=eps_t[:], func=ACT.Abs_reciprocal_sqrt)
@@ -414,6 +420,7 @@ def tile_multiheadlatentattention_pb_t_kernel(tc, x, w_kva, kva_norm_w, w_kvb, o
             if is_pair(n - 3):
                 stage2(old, 0, 0)
                 copy_out(old[0], 0, "S")
+                store_k(n - 3, 0, 1)
             if is_pair(n + 1):
                 x_quantise(n + 1)
             if is_pair(n):
@@ -428,7 +435,7 @@ def tile_multiheadlatentattention_pb_t_kernel(tc, x, w_kva, kva_norm_w, w_kvb, o
                 store_v(n - 3)
                 stage2(old, 1, 0)
                 copy_out(old[1], 0, "S")
-                store_k(n - 3)
+                store_k(n - 3, 1, 2)
             if n == 0:
                 quantise(wr_q[:], wr_s[:], wr_grp[:])
             if n < 2:

@@ -377,6 +377,9 @@ def tile_multiheadlatentattention_pb_t_kernel(tc, x, w_kva, kva_norm_w, w_kvb, o
         def is_pair(q):
             return 0 <= q < N_PAIRS
 
+        warm_ps = bank([P, 512], "warm_ps")
+        for i in range(3):
+            nc.tensor.matmul(out=warm_ps[:, 0:P], lhsT=ident[:], rhs=ident[:], start=True, stop=True)
         wa0 = wa_transpose(0)
         wa1 = wa_transpose(1)
         x_transpose(0, 0)
@@ -424,11 +427,10 @@ def tile_multiheadlatentattention_pb_t_kernel(tc, x, w_kva, kva_norm_w, w_kvb, o
             if is_pair(n + 1):
                 x_quantise(n + 1)
             if is_pair(n):
-                stage1_latent(n, 1)
-                stage1_latent(n, 0)
-                squares(n, 1)
-                squares(n, 0)
-                inverse_rms(n, 1)
+                for a in range(2):
+                    stage1_latent(n, a)
+                    squares(n, a)
+                inverse_rms(n, 0)
             if is_pair(n - 3):
                 stage2(old, 1, 1)
                 copy_out(old[1], 1, "V")
@@ -441,11 +443,11 @@ def tile_multiheadlatentattention_pb_t_kernel(tc, x, w_kva, kva_norm_w, w_kvb, o
             if n < 2:
                 wb_start(2 * n, "S")
             if is_pair(n):
-                inverse_rms(n, 0)
-                normalise(n, 1)
+                inverse_rms(n, 1)
+                normalise(n, 0)
             if n < 2:
                 wb_start(2 * n + 1, "V")
                 wb_quantise(2 * n)
                 wb_quantise(2 * n + 1)
             if is_pair(n):
-                normalise(n, 0)
+                normalise(n, 1)

@@ -377,9 +377,6 @@ def tile_multiheadlatentattention_pb_t_kernel(tc, x, w_kva, kva_norm_w, w_kvb, o
         def is_pair(q):
             return 0 <= q < N_PAIRS
 
-        warm_ps = bank([P, 512], "warm_ps")
-        for i in range(3):
-            nc.tensor.matmul(out=warm_ps[:, 0:P], lhsT=ident[:], rhs=ident[:], start=True, stop=True)
         wa0 = wa_transpose(0)
         wa1 = wa_transpose(1)
         x_transpose(0, 0)
@@ -413,6 +410,7 @@ def tile_multiheadlatentattention_pb_t_kernel(tc, x, w_kva, kva_norm_w, w_kvb, o
             if is_pair(n - 3):
                 stage2(old, 0, 1)
                 copy_out(old[0], 1, "V")
+                store_v(n - 3, 0, 1)
             if is_pair(n - 2):
                 stage1_rotary(n - 2)
                 rotate(n - 2)
@@ -434,7 +432,7 @@ def tile_multiheadlatentattention_pb_t_kernel(tc, x, w_kva, kva_norm_w, w_kvb, o
             if is_pair(n - 3):
                 stage2(old, 1, 1)
                 copy_out(old[1], 1, "V")
-                store_v(n - 3)
+                store_v(n - 3, 1, 2)
                 stage2(old, 1, 0)
                 copy_out(old[1], 0, "S")
                 store_k(n - 3, 1, 2)

@@ -14,13 +14,14 @@ ACT = mybir.ActivationFunctionType
 
 P = 128
 B, T, C = 4, 1024, 1024
-KVL, R, H = 512, 128, 4
+KVL, R, H, VD = 512, 128, 4, 128
+HALF = R // 2
 TPP = 8
 N_PAIRS = B * TPP // 2
 EPS = 1e-6
-RATIO = 10000.0 ** (-1.0 / 64.0)
+RATIO = 10000.0 ** (-1.0 / HALF)
 
-FLOPS = 2 * B * T * C * (KVL + R) + 2 * B * T * KVL * (H * 256)
+FLOPS = 2 * B * T * C * (KVL + R) + 2 * B * T * KVL * (H * (R + VD))
 
 
 def tile_multiheadlatentattention_pb_t_kernel(tc, x, w_kva, kva_norm_w, w_kvb, out_0, out_1):
@@ -30,18 +31,13 @@ def tile_multiheadlatentattention_pb_t_kernel(tc, x, w_kva, kva_norm_w, w_kvb, o
     ) as ring, tc.tile_pool(name="work", bufs=3) as work, tc.tile_pool(name="small", bufs=4) as small, tc.tile_pool(
         name="outp", bufs=5
     ) as outp, tc.psum_pool(name="psum", bufs=1) as psum, tc.manual_schedule():
-        engines = {"S": nc.scalar.copy, "V": nc.vector.tensor_copy}
+        copy_on = {"scalar": nc.scalar.copy, "vector": nc.vector.tensor_copy}
         live = {}
+        taken = {"latent": 0, "other": 0}
 
-        state = {"g": 0, "l": 0}
-
-        def bank(shape, name, tag="G"):
-            if tag == "G":
-                tag = "G%d" % (state["g"] % 5)
-                state["g"] = state["g"] + 1
-            if tag == "L":
-                tag = "L%d" % (state["l"] % 3)
-                state["l"] = state["l"] + 1
+        def psum_bank(shape, name, kind="other"):
+            tag = "%s%d" % (kind, taken[kind] % {"latent": 3, "other": 5}[kind])
+            taken[kind] = taken[kind] + 1
             return psum.tile(shape, F32, name=name, tag=tag)
 
         pos_i = const.tile([P, TPP], I32, name="pos_i")
@@ -58,39 +54,46 @@ def tile_multiheadlatentattention_pb_t_kernel(tc, x, w_kva, kva_norm_w, w_kvb, o
         x_rows = x.rearrange("b (p t) k -> b p (t k)", t=TPP)
         k_rows = out_0.rearrange("b (p t) h d -> b p t (h d)", t=TPP)
         v_rows = out_1.rearrange("b (p t) h d -> b p t (h d)", t=TPP)
-        wa_rows = w_kva[0:KVL, :].rearrange("(m s) k -> m s k", s=4)
+        wl_rows = w_kva[0:KVL, :].rearrange("(m s) k -> m s k", s=4)
         x_words = {}
 
         def load_x(t, tiles):
-            xr = const.tile([P, tiles * C], BF16, name="x_%d" % t)
-            nc.sync.dma_start(out=xr[:], in_=x_rows[t // TPP][:, C * (t % TPP) : C * (t % TPP + tiles)])
-            words = xr[:].bitcast(F32)
+            raw = const.tile([P, tiles * C], BF16, name="x_%d" % t)
+            nc.sync.dma_start(out=raw[:], in_=x_rows[t // TPP][:, C * (t % TPP) : C * (t % TPP + tiles)])
+            words = raw[:].bitcast(F32)
             for i in range(tiles):
                 x_words[t + i] = words[:, 512 * i : 512 * i + 512]
 
-        wa_words = []
+        wl_words = []
         for s in range(4):
-            wa_raw = const.tile([P, C], BF16, name="wa_raw%d" % s)
-            nc.sync.dma_start(out=wa_raw[:], in_=wa_rows[:, s, :])
-            wa_words.append(wa_raw[:].bitcast(F32))
+            wl_raw = const.tile([P, C], BF16, name="wl_raw%d" % s)
+            nc.sync.dma_start(out=wl_raw[:], in_=wl_rows[:, s, :])
+            wl_words.append(wl_raw[:].bitcast(F32))
             if s == 1:
                 nc.sync.dma_start(out=g_row[0:1, :], in_=kva_norm_w.rearrange("(o k) -> o k", o=1))
         load_x(0, 1)
         load_x(1, 1)
         wr_raw = const.tile([P, C], BF16, name="wr_raw")
         nc.sync.dma_start(out=wr_raw[:], in_=w_kva[KVL : KVL + R, :])
-        load_x(2, 2)
         wb_raw = const.tile([P, 8 * KVL], BF16, name="wb_raw")
-        nc.sync.dma_start(
-            out=wb_raw[:].rearrange("p (r k) -> p r k", r=8), in_=w_kvb.rearrange("(r p) k -> p r k", p=P)
-        )
+
+        def load_wb(half):
+            heads = slice(2 * half, 2 * half + 2)
+            nc.sync.dma_start(
+                out=wb_raw[:].rearrange("p (h k) -> p h k", h=H)[:, heads],
+                in_=w_kvb.rearrange("(h p i) k -> p h (i k)", p=P, i=2)[:, heads],
+            )
+
+        load_x(2, 2)
+        load_wb(0)
         load_x(4, 2)
+        load_wb(1)
         load_x(6, 2)
         for t in range(8, 2 * N_PAIRS, 4):
             load_x(t, 4)
 
-        tab = const.tile([P, TPP, 3, 64], F32, name="tab")
-        turns = const.tile([P, TPP, 64], F32, name="turns")
+        table = const.tile([P, TPP, 3, HALF], F32, name="table")
+        turns = const.tile([P, TPP, HALF], F32, name="turns")
         for s in range(4):
             nc.vector.tensor_scalar(
                 out=turns[:, :, s], in0=pos_i[:], scalar1=RATIO**s / (2.0 * math.pi), scalar2=None, op0=ALU.mult
@@ -104,113 +107,117 @@ def tile_multiheadlatentattention_pb_t_kernel(tc, x, w_kva, kva_norm_w, w_kvb, o
                     scalar2=None,
                     op0=ALU.mult,
                 )
-        whole = const.tile([P, TPP, 64], I32, name="whole")
+        whole = const.tile([P, TPP, HALF], I32, name="whole")
         nc.vector.tensor_copy(out=whole[:], in_=turns[:])
-        frac = const.tile([P, TPP, 64], F32, name="frac")
+        frac = const.tile([P, TPP, HALF], F32, name="frac")
         nc.vector.tensor_tensor(out=frac[:], in0=turns[:], in1=whole[:], op=ALU.subtract)
-        sin_h = const.tile([P, TPP, 64], F32, name="sin_h")
+        sin_h = const.tile([P, TPP, HALF], F32, name="sin_h")
         nc.scalar.activation(out=sin_h[:], in_=frac[:], func=ACT.Sin, scale=math.pi)
-        nc.scalar.activation(out=tab[:, :, 2, :], in_=frac[:], func=ACT.Sin, scale=2.0 * math.pi)
-        sq_h = const.tile([P, TPP, 64], F32, name="sq_h")
+        nc.scalar.activation(out=table[:, :, 2, :], in_=frac[:], func=ACT.Sin, scale=2.0 * math.pi)
+        sq_h = const.tile([P, TPP, HALF], F32, name="sq_h")
 
         def finish_tables():
             nc.vector.scalar_tensor_tensor(
                 out=sq_h[:], in0=sin_h[:], scalar=-2.0, in1=sin_h[:], op0=ALU.mult, op1=ALU.mult
             )
             nc.vector.tensor_scalar(
-                out=tab[:, :, 0, :], in0=tab[:, :, 2, :], scalar1=-1.0, scalar2=None, op0=ALU.mult
+                out=table[:, :, 0, :], in0=table[:, :, 2, :], scalar1=-1.0, scalar2=None, op0=ALU.mult
             )
-            nc.vector.tensor_scalar(out=tab[:, :, 1, :], in0=sq_h[:], scalar1=1.0, scalar2=None, op0=ALU.add)
+            nc.vector.tensor_scalar(out=table[:, :, 1, :], in0=sq_h[:], scalar1=1.0, scalar2=None, op0=ALU.add)
 
         wl_q = const.tile([P, 2 * KVL], U32, name="wl_q", align_bytes=256)
         wl_s = const.tile([P, 2 * KVL], U8, name="wl_s", align_bytes=256)
         wr_q = const.tile([P, 2 * R], U32, name="wr_q", align_bytes=256)
         wr_s = const.tile([P, 2 * R], U8, name="wr_s", align_bytes=256)
-        wb_q = const.tile([P, 1024], U32, name="wb_q", align_bytes=256)
-        wb_s = const.tile([P, 1024], U8, name="wb_s", align_bytes=256)
-        g_bc = const.tile([P, KVL], BF16, name="g_bc")
+        wb_q = const.tile([P, H * (R + VD)], U32, name="wb_q", align_bytes=256)
+        wb_s = const.tile([P, H * (R + VD)], U8, name="wb_s", align_bytes=256)
+        gain = const.tile([P, KVL], BF16, name="gain")
 
-        def transposes(blocks, name, tag="G"):
-            ps = bank([P, 512], name, tag)
+        def transpose_into(bank, i, words):
+            nc.tensor.transpose(out=bank[:, P * i : P * i + P], in_=words, identity=ident[:])
+
+        def transposed(blocks, name):
+            bank = psum_bank([P, 512], name)
             for i, words in enumerate(blocks):
-                nc.tensor.transpose(out=ps[:, P * i : P * i + P], in_=words, identity=ident[:])
-            return ps
+                transpose_into(bank, i, words)
+            return bank
 
-        def every_2nd(words, at):
+        def even_odd(words, at):
             return [words[:, at + v : at + 256 : 2] for v in range(2)]
 
-        def interleave(ps, dst, eng):
-            engines[eng](
+        def side_by_side(bank, dst, engine):
+            copy_on[engine](
                 out=dst.bitcast(F32).rearrange("p (g w v) -> p g w v", g=2, v=2),
-                in_=ps[:].rearrange("p (g v w) -> p g w v", g=2, v=2),
+                in_=bank[:].rearrange("p (g v w) -> p g w v", g=2, v=2),
             )
 
         def quantise(codes, scales, src):
             nc.vector.quantize_mx(out=codes.bitcast(FP8X4), scales=scales, in_=src)
 
-        def wa_transpose(u):
-            banks = [bank([P, 512], "wa_ps") for g in range(2)]
+        def weight_group():
+            return stage.tile([P, 1024], BF16, name="wgrp", tag="wgrp", align_bytes=64)
+
+        def wl_transpose(u):
+            banks = [psum_bank([P, 512], "wl_ps") for g in range(2)]
             for e in range(2):
                 for g in range(2):
-                    for v, words in enumerate(every_2nd(wa_words[2 * u + e], 256 * g)):
-                        nc.tensor.transpose(
-                            out=banks[g][:, P * (2 * e + v) : P * (2 * e + v) + P], in_=words, identity=ident[:]
-                        )
+                    for v, words in enumerate(even_odd(wl_words[2 * u + e], 256 * g)):
+                        transpose_into(banks[g], 2 * e + v, words)
             return banks
 
-        def wa_copy(ps, eng):
-            grp = stage.tile([P, 1024], BF16, name="wgrp", tag="wgrp", align_bytes=64)
-            engines[eng](
+        def wl_copy(bank, engine):
+            grp = weight_group()
+            copy_on[engine](
                 out=grp[:].bitcast(F32).rearrange("p (m e v) -> p m e v", e=2, v=2),
-                in_=ps[:].rearrange("p (e v m) -> p m e v", e=2, v=2),
+                in_=bank[:].rearrange("p (e v m) -> p m e v", e=2, v=2),
             )
             return grp
 
-        def wa_quantise(u, g, grp):
+        def wl_quantise(u, g, grp):
             cols = slice(KVL * g + 256 * u, KVL * g + 256 * u + 256)
             quantise(wl_q[:, cols], wl_s[:, cols], grp[:])
 
-        def wr_transpose():
+        def wr_group():
             words = wr_raw[:].bitcast(F32)
-            return transposes(every_2nd(words, 0) + every_2nd(words, 256), "wr_ps")
-
-        def wr_copy(ps, eng):
-            grp = stage.tile([P, 1024], BF16, name="wgrp", tag="wgrp", align_bytes=64)
-            interleave(ps, grp[:], eng)
+            bank = transposed(even_odd(words, 0) + even_odd(words, 256), "wr_ps")
+            grp = weight_group()
+            side_by_side(bank, grp[:], "vector")
             return grp
 
-        def wb_start(i, eng):
-            words = wb_raw[:].bitcast(F32)
-            ra, rb = ((0, 2), (4, 6), (1, 3), (5, 7))[i]
-            ps = transposes(every_2nd(words, 256 * ra) + every_2nd(words, 256 * rb), "wb_ps")
-            grp = stage.tile([P, 1024], BF16, name="wgrp", tag="wgrp", align_bytes=64)
-            interleave(ps, grp[:], eng)
-            live["wb", i] = grp
+        def wb_group(h, engine):
+            words = wb_raw[:].bitcast(F32)[:, 512 * h : 512 * h + 512]
+            bank = transposed(even_odd(words, 0) + even_odd(words, 256), "wb_ps")
+            grp = weight_group()
+            copy_on[engine](
+                out=grp[:].bitcast(F32).rearrange("p (m e v) -> p m e v", e=2, v=2),
+                in_=bank[:].rearrange("p (e v m) -> p m e v", e=2, v=2),
+            )
+            return grp
 
-        def wb_quantise(i):
-            cols = slice(256 * i, 256 * i + 256)
-            quantise(wb_q[:, cols], wb_s[:, cols], live["wb", i][:])
+        def wb_quantise(h, grp):
+            for part in range(2):
+                cols = slice(512 * part + P * h, 512 * part + P * h + P)
+                quantise(wb_q[:, cols], wb_s[:, cols], grp[:, 512 * part : 512 * part + 512])
 
-        def gain_spread():
-            g_ps = bank([P, KVL], "g_ps")
+        def spread_gain():
+            g_ps = psum_bank([P, KVL], "g_ps")
             nc.tensor.matmul(out=g_ps[:], lhsT=ones[:], rhs=g_row[:], start=True, stop=True)
             return g_ps
 
-        def gain_copy(g_ps):
+        def copy_gain(g_ps):
             nc.vector.tensor_copy(
-                out=g_bc[:].rearrange("p (u m e) -> p u m e", u=2, e=2),
+                out=gain[:].rearrange("p (u m e) -> p u m e", u=2, e=2),
                 in_=g_ps[:].rearrange("p (m u e) -> p u m e", u=2, e=2),
             )
 
         def x_transpose(q, a):
             words = x_words[2 * q + a]
-            live["xt", q, a] = transposes(every_2nd(words, 0) + every_2nd(words, 256), "xt")
+            live["xt", q, a] = transposed(even_odd(words, 0) + even_odd(words, 256), "xt")
 
-        def x_copy(q, a, eng):
-            if ("xg", q) not in live:
-                xg = stage.tile([P, 2048], BF16, name="xg", tag="xgrp", align_bytes=64)
-                live["xg", q] = xg
-            interleave(live["xt", q, a], live["xg", q][:, 1024 * a : 1024 * a + 1024], eng)
+        def x_copy(q, a):
+            if a == 0:
+                live["xg", q] = stage.tile([P, 2048], BF16, name="xg", tag="xgrp", align_bytes=64)
+            side_by_side(live["xt", q, a], live["xg", q][:, 1024 * a : 1024 * a + 1024], "scalar")
 
         def x_quantise(q):
             xq = ring.tile([P, 512], U32, name="xq", tag="xq", align_bytes=256)
@@ -220,11 +227,11 @@ def tile_multiheadlatentattention_pb_t_kernel(tc, x, w_kva, kva_norm_w, w_kvb, o
 
         def stage1_pass(out, q, a, g, codes, scales):
             xq, xs = live["xq", q]
-            xc = slice(256 * a + P * g, 256 * a + P * g + P)
+            cols = slice(256 * a + P * g, 256 * a + P * g + P)
             nc.tensor.matmul_mx(
                 out=out,
-                lhsT=xq[:, xc].bitcast(FP8X4),
-                lhsT_scale=xs[:, xc],
+                lhsT=xq[:, cols].bitcast(FP8X4),
+                lhsT_scale=xs[:, cols],
                 rhs=codes.bitcast(FP8X4),
                 rhs_scale=scales,
                 start=(g == 0),
@@ -232,14 +239,14 @@ def tile_multiheadlatentattention_pb_t_kernel(tc, x, w_kva, kva_norm_w, w_kvb, o
             )
 
         def stage1_latent(q, a):
-            l = bank([P, KVL], "l", "L")
+            l = psum_bank([P, KVL], "l", "latent")
             for g in range(2):
                 cols = slice(KVL * g, KVL * g + KVL)
                 stage1_pass(l[:], q, a, g, wl_q[:, cols], wl_s[:, cols])
             live["l", q, a] = l
 
         def stage1_rotary(q):
-            r_ps = bank([P, 2, R], "r_ps")
+            r_ps = psum_bank([P, 2, R], "r_ps")
             for a in range(2):
                 for g in range(2):
                     cols = slice(R * g, R * g + R)
@@ -269,159 +276,132 @@ def tile_multiheadlatentattention_pb_t_kernel(tc, x, w_kva, kva_norm_w, w_kvb, o
                 out=c_sb[:],
                 in0=live["l", q, a][:],
                 scalar=live["rstd", q, a][:],
-                in1=g_bc[:],
+                in1=gain[:],
                 op0=ALU.mult,
                 op1=ALU.mult,
             )
-            live["c", 2 * q + a] = c_sb
+            live["c", q, a] = c_sb
 
-        def c_transpose(tiles):
-            blocks = []
-            for t in tiles:
-                words = live["c", t][:].bitcast(F32)
-                blocks = blocks + [words[:, P * v : P * v + P] for v in range(2)]
-            live["ct", tiles] = transposes(blocks, "ct")
+        def c_transpose(q):
+            words = [live["c", q, a][:].bitcast(F32) for a in range(2)]
+            live["ct", q] = transposed([words[a][:, P * u : P * u + P] for a in range(2) for u in range(2)], "ct")
 
-        def c_copy(tiles, eng):
-            w = len(tiles)
+        def c_copy(q):
             grp = stage.tile([P, 1024], BF16, name="cgrp", tag="cgrp", align_bytes=64)
-            engines[eng](
-                out=grp[:, 0 : 512 * w].bitcast(F32).rearrange("p (g w v) -> p g w v", g=w, v=2),
-                in_=live["ct", tiles][:, 0 : 256 * w].rearrange("p (g v w) -> p g w v", g=w, v=2),
-            )
-            live["cg", tiles] = grp
+            side_by_side(live["ct", q], grp[:], "scalar")
+            live["cg", q] = grp
 
-        def c_quantise(tiles):
-            w = len(tiles)
+        def c_quantise(q):
             cq = work.tile([P, 256], U32, name="cq", tag="cq", align_bytes=256)
             cs = work.tile([P, 256], U8, name="cs", tag="cs", align_bytes=256)
-            quantise(cq[:, 0 : P * w], cs[:, 0 : P * w], live["cg", tiles][:, 0 : 512 * w])
-            live["cq", tiles] = (cq, cs)
+            quantise(cq[:], cs[:], live["cg", q][:])
+            live["cq", q] = (cq, cs)
 
-        def stage2(tiles, i, part):
-            cq, cs = live["cq", tiles]
-            kv = bank([P, 512], "kv")
+        def stage2(q, a, part):
+            cq, cs = live["cq", q]
+            kv = psum_bank([P, 512], "kv")
             nc.tensor.matmul_mx(
                 out=kv[:],
-                lhsT=cq[:, P * i : P * i + P].bitcast(FP8X4),
-                lhsT_scale=cs[:, P * i : P * i + P],
+                lhsT=cq[:, P * a : P * a + P].bitcast(FP8X4),
+                lhsT_scale=cs[:, P * a : P * a + P],
                 rhs=wb_q[:, 512 * part : 512 * part + 512].bitcast(FP8X4),
                 rhs_scale=wb_s[:, 512 * part : 512 * part + 512],
                 start=True,
                 stop=True,
             )
-            live["kv", tiles[i], part] = kv
+            return kv
 
-        def rotate(q):
-            t0 = 2 * (q % 4)
+        def products(q):
+            t0 = 2 * (q % (TPP // 2))
             r_pairs = live["r", q][:].rearrange("p t (j e) -> p t e j", e=2)
-            products = []
+            both = []
             for e in range(2):
-                m = work.tile([P, 2, 2, 64], F32, name="m", tag="m%d" % e)
+                m = work.tile([P, 2, 2, HALF], F32, name="m", tag="m%d" % e)
                 nc.vector.tensor_tensor(
                     out=m[:],
-                    in0=r_pairs[:, :, e : e + 1, :].to_broadcast([P, 2, 2, 64]),
-                    in1=tab[:, t0 : t0 + 2, 1 - e : 3 - e, :],
+                    in0=r_pairs[:, :, e : e + 1, :].to_broadcast([P, 2, 2, HALF]),
+                    in1=table[:, t0 : t0 + 2, 1 - e : 3 - e, :],
                     op=ALU.mult,
                 )
-                products.append(m)
-            live["m", q] = products
+                both.append(m)
+            live["m", q] = both
 
-        def open_out(q):
-            k_sb = outp.tile([P, 2, H, 256], F32, name="k_sb", tag="k_sb")
-            v_sb = outp.tile([P, 2, H * 128], F32, name="v_sb", tag="v_sb")
+        def rotary_key(q):
+            k_sb = outp.tile([P, 2, H, R + R], F32, name="k_sb", tag="k_sb")
+            v_sb = outp.tile([P, 2, H * VD], F32, name="v_sb", tag="v_sb")
             live["out", q] = (k_sb, v_sb)
-
-        def rotate_add(q, eng):
-            k_sb = live["out", q][0]
-            products = live["m", q]
-            eng.tensor_tensor(
-                out=k_sb[:, :, 0, 128:256].rearrange("p t (j e) -> p t j e", e=2),
-                in0=products[0][:].rearrange("p t e j -> p t j e"),
-                in1=products[1][:].rearrange("p t e j -> p t j e"),
+            m0, m1 = live["m", q]
+            nc.gpsimd.tensor_tensor(
+                out=k_sb[:, :, 0, R : R + R].rearrange("p t (j e) -> p t j e", e=2),
+                in0=m0[:].rearrange("p t e j -> p t j e"),
+                in1=m1[:].rearrange("p t e j -> p t j e"),
                 op=ALU.add,
             )
-
-        def rotate_spread(q, heads):
-            k_sb = live["out", q][0]
-            for h0, h1 in heads:
-                nc.gpsimd.tensor_scalar(
-                    out=k_sb[:, :, h0:h1, 128:256],
-                    in0=k_sb[:, :, 0:1, 128:256].to_broadcast([P, 2, h1 - h0, 128]),
-                    scalar1=1.0,
-                    scalar2=0.0,
-                    op0=ALU.mult,
-                    op1=ALU.add,
-                )
-
-        def copy_out(t, part, eng):
-            k_sb, v_sb = live["out", t // 2]
-            a = t % 2
-            kv = live["kv", t, part]
-            if part == 0:
-                engines[eng](out=k_sb[:, a, :, 0:128], in_=kv[:].rearrange("p (h d) -> p h d", h=H))
-            else:
-                engines[eng](out=v_sb[:, a, :], in_=kv[:])
-
-        def store_k(q, a0=0, a1=2):
-            t0 = 2 * (q % 4)
-            nc.sync.dma_start(
-                out=k_rows[q // 4][:, t0 + a0 : t0 + a1, :],
-                in_=live["out", q][0][:, a0:a1].rearrange("p t h d -> p t (h d)"),
+            nc.gpsimd.tensor_scalar(
+                out=k_sb[:, :, 1:H, R : R + R],
+                in0=k_sb[:, :, 0:1, R : R + R].to_broadcast([P, 2, H - 1, R]),
+                scalar1=1.0,
+                scalar2=0.0,
+                op0=ALU.mult,
+                op1=ALU.add,
             )
 
-        def store_v(q, a0=0, a1=2):
-            t0 = 2 * (q % 4)
-            nc.sync.dma_start(out=v_rows[q // 4][:, t0 + a0 : t0 + a1, :], in_=live["out", q][1][:, a0:a1, :])
+        def key_out(q, a):
+            kv = stage2(q, a, 0)
+            k_sb = live["out", q][0]
+            t = 2 * (q % (TPP // 2)) + a
+            nc.scalar.copy(out=k_sb[:, a, :, 0:R], in_=kv[:].rearrange("p (h d) -> p h d", h=H))
+            nc.sync.dma_start(
+                out=k_rows[q // (TPP // 2)][:, t : t + 1, :],
+                in_=k_sb[:, a : a + 1].rearrange("p t h d -> p t (h d)"),
+            )
+
+        def v_out(q, a):
+            kv = stage2(q, a, 1)
+            v_sb = live["out", q][1]
+            t = 2 * (q % (TPP // 2)) + a
+            nc.vector.tensor_copy(out=v_sb[:, a, :], in_=kv[:])
+            nc.sync.dma_start(out=v_rows[q // (TPP // 2)][:, t : t + 1, :], in_=v_sb[:, a : a + 1, :])
 
         def is_pair(q):
             return 0 <= q < N_PAIRS
 
-        wa0 = wa_transpose(0)
-        wa1 = wa_transpose(1)
+        wl_banks = [wl_transpose(u) for u in range(2)]
         x_transpose(0, 0)
-        grp0 = [wa_copy(wa0[g], "V") for g in range(2)]
+        groups = [wl_copy(wl_banks[0][g], "vector") for g in range(2)]
         for g in range(2):
-            wa_quantise(0, g, grp0[g])
-        grp1 = [wa_copy(wa1[g], "SV"[g]) for g in range(2)]
-        x_copy(0, 0, "S")
+            wl_quantise(0, g, groups[g])
+        groups = [wl_copy(wl_banks[1][g], ("scalar", "vector")[g]) for g in range(2)]
+        x_copy(0, 0)
         x_transpose(0, 1)
-        x_copy(0, 1, "S")
+        x_copy(0, 1)
         for g in range(2):
-            wa_quantise(1, g, grp1[g])
+            wl_quantise(1, g, groups[g])
         x_quantise(0)
-        gain_ps = gain_spread()
-        warm = const.tile([P, 1], F32, name="warm")
-        nc.scalar.activation(out=warm[:], in_=eps_t[:], func=ACT.Abs_reciprocal_sqrt)
-        gain_copy(gain_ps)
-        wr_grp = wr_copy(wr_transpose(), "V")
+        gain_ps = spread_gain()
+        first_use = const.tile([P, 1], F32, name="first_use")
+        nc.scalar.activation(out=first_use[:], in_=eps_t[:], func=ACT.Abs_reciprocal_sqrt)
+        copy_gain(gain_ps)
+        wr_grp = wr_group()
         finish_tables()
 
         for n in range(N_PAIRS + 3):
-            prev = (2 * n - 4, 2 * n - 3)
-            old = (2 * n - 6, 2 * n - 5)
             if is_pair(n + 1):
                 for a in range(2):
                     x_transpose(n + 1, a)
-                    x_copy(n + 1, a, "S")
+                    x_copy(n + 1, a)
             if is_pair(n - 2):
-                c_transpose(prev)
-                c_copy(prev, "S")
+                c_transpose(n - 2)
+                c_copy(n - 2)
             if is_pair(n - 3):
-                stage2(old, 0, 1)
-                copy_out(old[0], 1, "V")
-                store_v(n - 3, 0, 1)
+                v_out(n - 3, 0)
             if is_pair(n - 2):
                 stage1_rotary(n - 2)
-                rotate(n - 2)
-                open_out(n - 2)
-                rotate_add(n - 2, nc.gpsimd)
-                rotate_spread(n - 2, [(1, 4)])
-                c_quantise(prev)
+                products(n - 2)
+                rotary_key(n - 2)
+                c_quantise(n - 2)
             if is_pair(n - 3):
-                stage2(old, 0, 0)
-                copy_out(old[0], 0, "S")
-                store_k(n - 3, 0, 1)
+                key_out(n - 3, 0)
             if is_pair(n + 1):
                 x_quantise(n + 1)
             if is_pair(n):
@@ -430,22 +410,18 @@ def tile_multiheadlatentattention_pb_t_kernel(tc, x, w_kva, kva_norm_w, w_kvb, o
                     squares(n, a)
                 inverse_rms(n, 0)
             if is_pair(n - 3):
-                stage2(old, 1, 1)
-                copy_out(old[1], 1, "V")
-                store_v(n - 3, 1, 2)
-                stage2(old, 1, 0)
-                copy_out(old[1], 0, "S")
-                store_k(n - 3, 1, 2)
+                v_out(n - 3, 1)
+                key_out(n - 3, 1)
             if n == 0:
                 quantise(wr_q[:], wr_s[:], wr_grp[:])
             if n < 2:
-                wb_start(2 * n, "S")
+                wb_first = wb_group(2 * n, "scalar")
             if is_pair(n):
                 inverse_rms(n, 1)
                 normalise(n, 0)
             if n < 2:
-                wb_start(2 * n + 1, "V")
-                wb_quantise(2 * n)
-                wb_quantise(2 * n + 1)
+                wb_second = wb_group(2 * n + 1, "vector")
+                wb_quantise(2 * n, wb_first)
+                wb_quantise(2 * n + 1, wb_second)
             if is_pair(n):
                 normalise(n, 1)

import math

import concourse.mybir as mybir
from concourse.masks import make_identity

F32 = mybir.dt.float32
BF16 = mybir.dt.bfloat16
I32 = mybir.dt.int32
U32 = mybir.dt.uint32
U8 = mybir.dt.uint8
FP8X4 = mybir.dt.float8_e4m3fn_x4
ALU = mybir.AluOpType
ACT = mybir.ActivationFunctionType

P = 128
B, T, C = 4, 1024, 1024
KVL, R, H, VD = 512, 128, 4, 128
HALF = R // 2
TPP = 8
N_PAIRS = B * TPP // 2
EPS = 1e-6
RATIO = 10000.0 ** (-1.0 / HALF)

FLOPS = 2 * B * T * C * (KVL + R) + 2 * B * T * KVL * (H * (R + VD))


def tile_multiheadlatentattention_pb_t_kernel(tc, x, w_kva, kva_norm_w, w_kvb, out_0, out_1):
    nc = tc.nc
    with tc.tile_pool(name="const", bufs=1) as const, tc.tile_pool(name="stage", bufs=3) as stage, tc.tile_pool(
        name="ring", bufs=6
    ) as ring, tc.tile_pool(name="work", bufs=3) as work, tc.tile_pool(name="small", bufs=4) as small, tc.tile_pool(
        name="outp", bufs=5
    ) as outp, tc.psum_pool(name="psum", bufs=1) as psum, tc.manual_schedule():
        copy_on = {"scalar": nc.scalar.copy, "vector": nc.vector.tensor_copy}
        live = {}
        taken = {"latent": 0, "other": 0}

        def psum_bank(shape, name, kind="other"):
            tag = "%s%d" % (kind, taken[kind] % {"latent": 3, "other": 5}[kind])
            taken[kind] = taken[kind] + 1
            return psum.tile(shape, F32, name=name, tag=tag)

        pos_i = const.tile([P, TPP], I32, name="pos_i")
        nc.gpsimd.iota(pos_i[:], pattern=[[1, TPP]], base=0, channel_multiplier=TPP)
        g_row = const.tile([P, KVL], BF16, name="g_row")
        nc.vector.memset(g_row[:], 0.0)
        ident = const.tile([P, P], F32, name="ident")
        make_identity(nc, ident[:])
        ones = const.tile([P, P], BF16, name="ones")
        nc.gpsimd.memset(ones[:], 1.0)
        eps_t = const.tile([P, 1], F32, name="eps_t")
        nc.vector.memset(eps_t[:], EPS)

        x_rows = x.rearrange("b (p t) k -> b p (t k)", t=TPP)
        k_rows = out_0.rearrange("b (p t) h d -> b p t (h d)", t=TPP)
        v_rows = out_1.rearrange("b (p t) h d -> b p t (h d)", t=TPP)
        wl_rows = w_kva[0:KVL, :].rearrange("(m s) k -> m s k", s=4)
        x_words = {}

        def load_x(t, tiles):
            raw = const.tile([P, tiles * C], BF16, name="x_%d" % t)
            nc.sync.dma_start(out=raw[:], in_=x_rows[t // TPP][:, C * (t % TPP) : C * (t % TPP + tiles)])
            words = raw[:].bitcast(F32)
            for i in range(tiles):
                x_words[t + i] = words[:, 512 * i : 512 * i + 512]

        wl_words = []
        for s in range(4):
            wl_raw = const.tile([P, C], BF16, name="wl_raw%d" % s)
            nc.sync.dma_start(out=wl_raw[:], in_=wl_rows[:, s, :])
            wl_words.append(wl_raw[:].bitcast(F32))
            if s == 1:
                nc.sync.dma_start(out=g_row[0:1, :], in_=kva_norm_w.rearrange("(o k) -> o k", o=1))
        load_x(0, 1)
        load_x(1, 1)
        wr_raw = const.tile([P, C], BF16, name="wr_raw")
        nc.sync.dma_start(out=wr_raw[:], in_=w_kva[KVL : KVL + R, :])
        wb_raw = const.tile([P, 8 * KVL], BF16, name="wb_raw")

        def load_wb(half):
            heads = slice(2 * half, 2 * half + 2)
            nc.sync.dma_start(
                out=wb_raw[:].rearrange("p (h k) -> p h k", h=H)[:, heads],
                in_=w_kvb.rearrange("(h p i) k -> p h (i k)", p=P, i=2)[:, heads],
            )

        load_x(2, 2)
        load_wb(0)
        load_x(4, 2)
        load_wb(1)
        load_x(6, 2)
        for t in range(8, 2 * N_PAIRS, 4):
            load_x(t, 4)

        table = const.tile([P, TPP, 3, HALF], F32, name="table")
        turns = const.tile([P, TPP, HALF], F32, name="turns")
        for s in range(4):
            nc.vector.tensor_scalar(
                out=turns[:, :, s], in0=pos_i[:], scalar1=RATIO**s / (2.0 * math.pi), scalar2=None, op0=ALU.mult
            )
        for n in (4, 16):
            for s in range(1, 4):
                nc.vector.tensor_scalar(
                    out=turns[:, :, n * s : n * s + n],
                    in0=turns[:, :, 0:n],
                    scalar1=RATIO ** (n * s),
                    scalar2=None,
                    op0=ALU.mult,
                )
        whole = const.tile([P, TPP, HALF], I32, name="whole")
        nc.vector.tensor_copy(out=whole[:], in_=turns[:])
        frac = const.tile([P, TPP, HALF], F32, name="frac")
        nc.vector.tensor_tensor(out=frac[:], in0=turns[:], in1=whole[:], op=ALU.subtract)
        sin_h = const.tile([P, TPP, HALF], F32, name="sin_h")
        nc.scalar.activation(out=sin_h[:], in_=frac[:], func=ACT.Sin, scale=math.pi)
        nc.scalar.activation(out=table[:, :, 2, :], in_=frac[:], func=ACT.Sin, scale=2.0 * math.pi)
        sq_h = const.tile([P, TPP, HALF], F32, name="sq_h")

        def finish_tables():
            nc.vector.scalar_tensor_tensor(
                out=sq_h[:], in0=sin_h[:], scalar=-2.0, in1=sin_h[:], op0=ALU.mult, op1=ALU.mult
            )
            nc.vector.tensor_scalar(
                out=table[:, :, 0, :], in0=table[:, :, 2, :], scalar1=-1.0, scalar2=None, op0=ALU.mult
            )
            nc.vector.tensor_scalar(out=table[:, :, 1, :], in0=sq_h[:], scalar1=1.0, scalar2=None, op0=ALU.add)

        wl_q = const.tile([P, 2 * KVL], U32, name="wl_q", align_bytes=256)
        wl_s = const.tile([P, 2 * KVL], U8, name="wl_s", align_bytes=256)
        wr_q = const.tile([P, 2 * R], U32, name="wr_q", align_bytes=256)
        wr_s = const.tile([P, 2 * R], U8, name="wr_s", align_bytes=256)
        wb_q = const.tile([P, H * (R + VD)], U32, name="wb_q", align_bytes=256)
        wb_s = const.tile([P, H * (R + VD)], U8, name="wb_s", align_bytes=256)
        gain = const.tile([P, KVL], BF16, name="gain")

        def transpose_into(bank, i, words):
            nc.tensor.transpose(out=bank[:, P * i : P * i + P], in_=words, identity=ident[:])

        def transposed(blocks, name):
            bank = psum_bank([P, 512], name)
            for i, words in enumerate(blocks):
                transpose_into(bank, i, words)
            return bank

        def even_odd(words, at):
            return [words[:, at + v : at + 256 : 2] for v in range(2)]

        def side_by_side(bank, dst, engine):
            copy_on[engine](
                out=dst.bitcast(F32).rearrange("p (g w v) -> p g w v", g=2, v=2),
                in_=bank[:].rearrange("p (g v w) -> p g w v", g=2, v=2),
            )

        def quantise(codes, scales, src):
            nc.vector.quantize_mx(out=codes.bitcast(FP8X4), scales=scales, in_=src)

        def weight_group():
            return stage.tile([P, 1024], BF16, name="wgrp", tag="wgrp", align_bytes=64)

        def wl_transpose(u):
            banks = [psum_bank([P, 512], "wl_ps") for g in range(2)]
            for e in range(2):
                for g in range(2):
                    for v, words in enumerate(even_odd(wl_words[2 * u + e], 256 * g)):
                        transpose_into(banks[g], 2 * e + v, words)
            return banks

        def wl_copy(bank, engine):
            grp = weight_group()
            copy_on[engine](
                out=grp[:].bitcast(F32).rearrange("p (m e v) -> p m e v", e=2, v=2),
                in_=bank[:].rearrange("p (e v m) -> p m e v", e=2, v=2),
            )
            return grp

        def wl_quantise(u, g, grp):
            cols = slice(KVL * g + 256 * u, KVL * g + 256 * u + 256)
            quantise(wl_q[:, cols], wl_s[:, cols], grp[:])

        def wr_group():
            words = wr_raw[:].bitcast(F32)
            bank = transposed(even_odd(words, 0) + even_odd(words, 256), "wr_ps")
            grp = weight_group()
            side_by_side(bank, grp[:], "vector")
            return grp

        def wb_group(h, engine):
            words = wb_raw[:].bitcast(F32)[:, 512 * h : 512 * h + 512]
            bank = transposed(even_odd(words, 0) + even_odd(words, 256), "wb_ps")
            grp = weight_group()
            copy_on[engine](
                out=grp[:].bitcast(F32).rearrange("p (m e v) -> p m e v", e=2, v=2),
                in_=bank[:].rearrange("p (e v m) -> p m e v", e=2, v=2),
            )
            return grp

        def wb_quantise(h, grp):
            for part in range(2):
                cols = slice(512 * part + P * h, 512 * part + P * h + P)
                quantise(wb_q[:, cols], wb_s[:, cols], grp[:, 512 * part : 512 * part + 512])

        def spread_gain():
            g_ps = psum_bank([P, KVL], "g_ps")
            nc.tensor.matmul(out=g_ps[:], lhsT=ones[:], rhs=g_row[:], start=True, stop=True)
            return g_ps

        def copy_gain(g_ps):
            nc.vector.tensor_copy(
                out=gain[:].rearrange("p (u m e) -> p u m e", u=2, e=2),
                in_=g_ps[:].rearrange("p (m u e) -> p u m e", u=2, e=2),
            )

        def x_transpose(q, a):
            words = x_words[2 * q + a]
            live["xt", q, a] = transposed(even_odd(words, 0) + even_odd(words, 256), "xt")

        def x_copy(q, a):
            if a == 0:
                live["xg", q] = stage.tile([P, 2048], BF16, name="xg", tag="xgrp", align_bytes=64)
            side_by_side(live["xt", q, a], live["xg", q][:, 1024 * a : 1024 * a + 1024], "scalar")

        def x_quantise(q):
            xq = ring.tile([P, 512], U32, name="xq", tag="xq", align_bytes=256)
            xs = ring.tile([P, 512], U8, name="xs", tag="xs", align_bytes=256)
            quantise(xq[:], xs[:], live["xg", q][:])
            live["xq", q] = (xq, xs)

        def stage1_pass(out, q, a, g, codes, scales):
            xq, xs = live["xq", q]
            cols = slice(256 * a + P * g, 256 * a + P * g + P)
            nc.tensor.matmul_mx(
                out=out,
                lhsT=xq[:, cols].bitcast(FP8X4),
                lhsT_scale=xs[:, cols],
                rhs=codes.bitcast(FP8X4),
                rhs_scale=scales,
                start=(g == 0),
                stop=(g == 1),
            )

        def stage1_latent(q, a):
            l = psum_bank([P, KVL], "l", "latent")
            for g in range(2):
                cols = slice(KVL * g, KVL * g + KVL)
                stage1_pass(l[:], q, a, g, wl_q[:, cols], wl_s[:, cols])
            live["l", q, a] = l

        def stage1_rotary(q):
            r_ps = psum_bank([P, 2, R], "r_ps")
            for a in range(2):
                for g in range(2):
                    cols = slice(R * g, R * g + R)
                    stage1_pass(r_ps[:, a, :], q, a, g, wr_q[:, cols], wr_s[:, cols])
            live["r", q] = r_ps

        def squares(q, a):
            ssq = small.tile([P, 1], F32, name="ssq", tag="ssq%d" % a)
            junk = work.tile([P, KVL], BF16, name="junk", tag="junk")
            nc.scalar.activation(out=junk[:], in_=live["l", q, a][:], func=ACT.Square, accum_out=ssq[:])
            live["ssq", q, a] = ssq

        def inverse_rms(q, a):
            rstd = small.tile([P, 1], F32, name="rstd", tag="rstd%d" % a)
            nc.scalar.activation(
                out=rstd[:],
                in_=live["ssq", q, a][:],
                func=ACT.Abs_reciprocal_sqrt,
                scale=1.0 / KVL,
                bias=eps_t[:, 0:1],
            )
            live["rstd", q, a] = rstd

        def normalise(q, a):
            c_sb = work.tile([P, KVL], BF16, name="c_sb", tag="c_sb", bufs=6)
            nc.vector.scalar_tensor_tensor(
                out=c_sb[:],
                in0=live["l", q, a][:],
                scalar=live["rstd", q, a][:],
                in1=gain[:],
                op0=ALU.mult,
                op1=ALU.mult,
            )
            live["c", q, a] = c_sb

        def c_transpose(q):
            words = [live["c", q, a][:].bitcast(F32) for a in range(2)]
            live["ct", q] = transposed([words[a][:, P * u : P * u + P] for a in range(2) for u in range(2)], "ct")

        def c_copy(q):
            grp = stage.tile([P, 1024], BF16, name="cgrp", tag="cgrp", align_bytes=64)
            side_by_side(live["ct", q], grp[:], "scalar")
            live["cg", q] = grp

        def c_quantise(q):
            cq = work.tile([P, 256], U32, name="cq", tag="cq", align_bytes=256)
            cs = work.tile([P, 256], U8, name="cs", tag="cs", align_bytes=256)
            quantise(cq[:], cs[:], live["cg", q][:])
            live["cq", q] = (cq, cs)

        def stage2(q, a, part):
            cq, cs = live["cq", q]
            kv = psum_bank([P, 512], "kv")
            nc.tensor.matmul_mx(
                out=kv[:],
                lhsT=cq[:, P * a : P * a + P].bitcast(FP8X4),
                lhsT_scale=cs[:, P * a : P * a + P],
                rhs=wb_q[:, 512 * part : 512 * part + 512].bitcast(FP8X4),
                rhs_scale=wb_s[:, 512 * part : 512 * part + 512],
                start=True,
                stop=True,
            )
            return kv

        def products(q):
            t0 = 2 * (q % (TPP // 2))
            r_pairs = live["r", q][:].rearrange("p t (j e) -> p t e j", e=2)
            both = []
            for e in range(2):
                m = work.tile([P, 2, 2, HALF], F32, name="m", tag="m%d" % e)
                nc.vector.tensor_tensor(
                    out=m[:],
                    in0=r_pairs[:, :, e : e + 1, :].to_broadcast([P, 2, 2, HALF]),
                    in1=table[:, t0 : t0 + 2, 1 - e : 3 - e, :],
                    op=ALU.mult,
                )
                both.append(m)
            live["m", q] = both

        def rotary_key(q):
            k_sb = outp.tile([P, 2, H, R + R], F32, name="k_sb", tag="k_sb")
            v_sb = outp.tile([P, 2, H * VD], F32, name="v_sb", tag="v_sb")
            live["out", q] = (k_sb, v_sb)
            m0, m1 = live["m", q]
            nc.gpsimd.tensor_tensor(
                out=k_sb[:, :, 0, R : R + R].rearrange("p t (j e) -> p t j e", e=2),
                in0=m0[:].rearrange("p t e j -> p t j e"),
                in1=m1[:].rearrange("p t e j -> p t j e"),
                op=ALU.add,
            )
            nc.gpsimd.tensor_scalar(
                out=k_sb[:, :, 1:H, R : R + R],
                in0=k_sb[:, :, 0:1, R : R + R].to_broadcast([P, 2, H - 1, R]),
                scalar1=1.0,
                scalar2=0.0,
                op0=ALU.mult,
                op1=ALU.add,
            )

        def key_out(q, a):
            kv = stage2(q, a, 0)
            k_sb = live["out", q][0]
            t = 2 * (q % (TPP // 2)) + a
            nc.scalar.copy(out=k_sb[:, a, :, 0:R], in_=kv[:].rearrange("p (h d) -> p h d", h=H))
            nc.sync.dma_start(
                out=k_rows[q // (TPP // 2)][:, t : t + 1, :],
                in_=k_sb[:, a : a + 1].rearrange("p t h d -> p t (h d)"),
            )

        def v_out(q, a):
            kv = stage2(q, a, 1)
            v_sb = live["out", q][1]
            t = 2 * (q % (TPP // 2)) + a
            nc.vector.tensor_copy(out=v_sb[:, a, :], in_=kv[:])
            nc.sync.dma_start(out=v_rows[q // (TPP // 2)][:, t : t + 1, :], in_=v_sb[:, a : a + 1, :])

        def is_pair(q):
            return 0 <= q < N_PAIRS

        wl_banks = [wl_transpose(u) for u in range(2)]
        x_transpose(0, 0)
        groups = [wl_copy(wl_banks[0][g], "vector") for g in range(2)]
        for g in range(2):
            wl_quantise(0, g, groups[g])
        groups = [wl_copy(wl_banks[1][g], ("scalar", "vector")[g]) for g in range(2)]
        x_copy(0, 0)
        x_transpose(0, 1)
        x_copy(0, 1)
        for g in range(2):
            wl_quantise(1, g, groups[g])
        x_quantise(0)
        gain_ps = spread_gain()
        first_use = const.tile([P, 1], F32, name="first_use")
        nc.scalar.activation(out=first_use[:], in_=eps_t[:], func=ACT.Abs_reciprocal_sqrt)
        copy_gain(gain_ps)
        wr_grp = wr_group()
        finish_tables()

        for n in range(N_PAIRS + 3):
            if is_pair(n + 1):
                for a in range(2):
                    x_transpose(n + 1, a)
                    x_copy(n + 1, a)
            if is_pair(n - 2):
                c_transpose(n - 2)
                c_copy(n - 2)
            if is_pair(n - 3):
                v_out(n - 3, 0)
            if is_pair(n - 2):
                stage1_rotary(n - 2)
                products(n - 2)
                rotary_key(n - 2)
                c_quantise(n - 2)
            if is_pair(n - 3):
                key_out(n - 3, 0)
            if is_pair(n + 1):
                x_quantise(n + 1)
            if is_pair(n):
                for a in range(2):
                    stage1_latent(n, a)
                    squares(n, a)
                inverse_rms(n, 0)
            if is_pair(n - 3):
                v_out(n - 3, 1)
                key_out(n - 3, 1)
            if n == 0:
                quantise(wr_q[:], wr_s[:], wr_grp[:])
            if n < 2:
                wb_first = wb_group(2 * n, "scalar")
            if is_pair(n):
                inverse_rms(n, 1)
                normalise(n, 0)
            if n < 2:
                wb_second = wb_group(2 * n + 1, "vector")
                wb_quantise(2 * n, wb_first)
                wb_quantise(2 * n + 1, wb_second)
            if is_pair(n):
                normalise(n, 1)
